import numpy as np
import ml_dtypes


def mxq(x, axis, fmt="e4m3"):
    dtype, down = {"e4m3": (ml_dtypes.float8_e4m3fn, 7), "e5m2": (ml_dtypes.float8_e5m2, 14)}[fmt]
    v = np.moveaxis(np.asarray(x, np.float32).astype(ml_dtypes.bfloat16).astype(np.float64), axis, -1)
    blocks = v.reshape(v.shape[:-1] + (-1, 32))
    amax = np.abs(blocks).max(-1, keepdims=True)
    byte = np.maximum(np.where(amax > 0, np.frexp(amax)[1] - 1 + 127, 0) - down, 1)
    scale = np.exp2(byte - 127.0)
    codes = (blocks / scale).astype(np.float32).astype(dtype).astype(np.float64)
    return np.moveaxis((codes * scale).reshape(v.shape), -1, axis)


WIDE = False


def mx_kscale(k):
    if not WIDE:
        return np.ones(k)
    levels = np.array([30, -30])
    if k % 512:
        return np.exp2(np.random.permutation(np.resize(levels, k // 32))).repeat(32)
    a = np.empty((k // 512, 16))
    for p in range(k // 512):
        a[p, :8] = np.random.permutation(np.resize(levels, 8))
        for g in range(8):
            far = levels[np.abs(levels - a[p, g]) >= 10]
            a[p, g + 8] = far[np.random.randint(len(far))]
    return np.exp2(a.ravel()).repeat(32)


BF16 = ml_dtypes.bfloat16


def bf(x):
    return np.asarray(x, np.float32).astype(BF16)


def f64(x):
    return np.asarray(x).astype(np.float64)


B, N, E, H, C = 1, 1024, 2048, 8, 512
D = E // H
THETA_SCALE = 1.0e4


def position_thetas():
    return np.repeat(1.0 / THETA_SCALE ** np.linspace(0.0, 1.0, D // 2), 2)


def multiply_by_i(t):
    return np.stack((-t[..., 1::2], t[..., ::2]), axis=-1).reshape(t.shape)


def setup_inputs():
    s = mx_kscale(E)
    return {"x": bf(np.random.standard_normal((B, N, E)) * s),
            "w": bf(np.random.standard_normal((E, E)) / np.sqrt(E) / s[:, None]),
            "b": bf(np.random.standard_normal(E) * 0.3)}


def reference(x, w, b):
    p = (mxq(f64(x), 2, "e5m2") @ mxq(f64(w), 0, "e4m3")) + f64(b)
    p = p.reshape(B, N, H, D).transpose(0, 2, 1, 3)
    pos = f64(np.arange(N))[:, None] * position_thetas()[None, :]
    return p * np.cos(pos)[None, None] + multiply_by_i(p) * np.sin(pos)[None, None]

@@ -1,0 +1,258 @@
+from contextlib import ExitStack
+import math
+
+import concourse.mybir as mybir
+from concourse.masks import make_identity
+
+N_TOK, E, H, D = 1024, 2048, 8, 256
+FLOPS = 2 * N_TOK * E * E
+
+F32 = mybir.dt.float32
+BF16 = mybir.dt.bfloat16
+I32 = mybir.dt.int32
+U32 = mybir.dt.uint32
+U8 = mybir.dt.uint8
+E4X4 = mybir.dt.float8_e4m3fn_x4
+E5X4 = mybir.dt.float8_e5m2_x4
+ALU = mybir.AluOpType
+ACT = mybir.ActivationFunctionType
+
+P = 128
+G = 4
+HALF = 512
+CHUNKS = ((0, 1), (1, 1), (2, 2), (4, 2), (6, 2))
+ADD_ON_GPSIMD = True
+
+
+def tile_multiscaleretention_pa_kernel(tc, x, w, b, out):
+    nc = tc.nc
+    with ExitStack() as ctx:
+        const = ctx.enter_context(tc.tile_pool(name="const", bufs=1))
+        wg_pool = ctx.enter_context(tc.tile_pool(name="wg", bufs=4))
+        wc_pool = ctx.enter_context(tc.tile_pool(name="wc", bufs=3))
+        ep3 = ctx.enter_context(tc.tile_pool(name="ep3", bufs=3))
+        ep2 = ctx.enter_context(tc.tile_pool(name="ep2", bufs=2))
+        acc_pool = ctx.enter_context(tc.psum_pool(name="acc", bufs=4))
+        tp_pool = ctx.enter_context(tc.psum_pool(name="tp", bufs=4))
+
+        ones = const.tile([P, 1], F32, name="ones")
+        nc.vector.memset(ones[:], 1.0)
+        scr = const.tile([P, 1], F32, name="scr")
+        nc.scalar.activation(out=scr[:], in_=ones[:], func=ACT.Sin, scale=1.0)
+
+        ident = const.tile([P, P], F32, name="ident")
+        make_identity(nc, ident[:])
+        n_iota = const.tile([P, N_TOK], F32, name="n_iota")
+        nc.gpsimd.iota(n_iota[:], pattern=[[HALF, 2], [1, 4], [4, P]], base=0,
+                       channel_multiplier=0, allow_small_or_imprecise_dtypes=True)
+
+        xv = x[0].rearrange("(s r i) k -> s r i k", s=2, i=4)
+        x_raw = {}
+        w_raw = {}
+        head_src = {}
+
+        def load_x(s, g):
+            t = const.tile([P, 4, 512], BF16, name="x_raw%d%d" % (s, g))
+            nc.sync.dma_start(out=t[:], in_=xv[s, :, :, 512 * g:512 * (g + 1)])
+            x_raw[(s, g)] = t
+
+        def load_w(c, g):
+            h0, nh = CHUNKS[c]
+            t = const.tile([P, 4, D * nh], BF16, name="w_raw%d%d" % (c, g))
+            nc.sync.dma_start(
+                out=t[:],
+                in_=w[512 * g:512 * (g + 1), D * h0:D * (h0 + nh)].rearrange("(p j) c -> p j c", j=4))
+            for hl in range(nh):
+                head_src[(h0 + hl, g)] = t[:, :, D * hl:D * (hl + 1)]
+
+        b_raw = const.tile([P, H, 2], BF16, name="b_raw")
+        for g in range(G):
+            load_x(0, g)
+            load_w(0, g)
+        nc.sync.dma_start(out=b_raw[:], in_=b.rearrange("(h j e) -> j h e", h=H, e=2))
+        for g in range(G):
+            load_x(1, g)
+        for c in range(1, len(CHUNKS)):
+            for g in range(G):
+                load_w(c, g)
+
+        ratio = 10000.0 ** (-1.0 / 127.0)
+        frow = const.tile([P, P], F32, name="frow")
+        nc.vector.tensor_scalar(out=frow[:, 0:1], in0=ones[:], scalar1=1.0 / (2.0 * math.pi),
+                                scalar2=None, op0=ALU.mult)
+        m = 1
+        while m < P:
+            nc.vector.tensor_scalar(out=frow[:, m:2 * m], in0=frow[:, 0:m], scalar1=ratio ** m,
+                                    scalar2=None, op0=ALU.mult)
+            m *= 2
+        fdiag = const.tile([P, P], F32, name="fdiag")
+        nc.vector.tensor_tensor(out=fdiag[:], in0=frow[:], in1=ident[:], op=ALU.mult)
+        fcol = const.tile([P, 1], F32, name="fcol")
+        nc.vector.tensor_reduce(out=fcol[:], in_=fdiag[:], axis=mybir.AxisListType.X, op=ALU.add)
+
+        xg = const.tile([P, G, 4 * HALF], BF16, name="xg", align_bytes=64)
+        xg_w = xg[:].bitcast(F32).rearrange("p g (c u) -> p g c u", u=2)
+        xc = [const.tile([P, G, HALF], U32, name="xc%d" % s, align_bytes=64) for s in range(2)]
+        xs = [const.tile([P, G, HALF], U8, name="xs%d" % s, align_bytes=64) for s in range(2)]
+
+        def x_prep(s, g):
+            words = x_raw[(s, g)][:].bitcast(F32)
+            for a in range(2):
+                xt = tp_pool.tile([P, 2, 2, P], F32, name="xt", tag="tp")
+                for ii in range(2):
+                    for u in range(2):
+                        nc.tensor.transpose(xt[:, ii, u, :], words[:, 2 * a + ii, u:256:2], ident[:])
+                dst = xg_w[:, g, 256 * a:256 * (a + 1), :].rearrange("p (i r) u -> p i r u", i=2)
+                src = xt[:].rearrange("p i u r -> p i r u")
+                nc.scalar.copy(out=dst, in_=src)
+
+        def x_quant(s, g):
+            nc.vector.quantize_mx(out=xc[s][:, g, :].bitcast(E5X4), scales=xs[s][:, g, :], in_=xg[:, g, :])
+
+        w_codes = {}
+        wg_tiles = {}
+
+        def w_interleave(h, g, eng):
+            if g % 2 == 0:
+                wg_tiles[(h, g // 2)] = wg_pool.tile([P, 2, 4 * D], BF16, name="wg", tag="wg", align_bytes=64)
+            t = wg_tiles[(h, g // 2)]
+            dst = t[:, g % 2, :].rearrange("p (e j t) -> p e j t", e=2, t=4)
+            src = head_src[(h, g)].rearrange("p t (j e) -> p e j t", e=2)
+            if eng == "s":
+                nc.scalar.copy(out=dst, in_=src)
+            else:
+                nc.vector.tensor_copy(out=dst, in_=src)
+
+        def w_tiles(h):
+            cod = wc_pool.tile([P, G, D], U32, name="wcod", tag="wcod", align_bytes=64)
+            sca = wc_pool.tile([P, G, D], U8, name="wsca", tag="wsca", align_bytes=64)
+            w_codes[h] = (cod, sca)
+
+        def w_quant1(h, g):
+            cod, sca = w_codes[h]
+            nc.vector.quantize_mx(out=cod[:, g, :].bitcast(E4X4), scales=sca[:, g, :],
+                                  in_=wg_tiles[(h, g // 2)][:, g % 2, :])
+
+        def w_quant2(h, a):
+            cod, sca = w_codes[h]
+            nc.vector.quantize_mx(
+                out=cod[:, 2 * a:2 * a + 2, :].rearrange("p g c -> p (g c)").bitcast(E4X4),
+                scales=sca[:, 2 * a:2 * a + 2, :].rearrange("p g c -> p (g c)"),
+                in_=wg_tiles[(h, a)][:].rearrange("p g c -> p (g c)"))
+
+        cos_t = const.tile([P, N_TOK], F32, name="cos_t")
+        sin_t = const.tile([P, N_TOK], F32, name="sin_t")
+        b_f = const.tile([P, H, 2], F32, name="b_f")
+
+        def tables():
+            turns = const.tile([P, N_TOK], F32, name="turns")
+            whole_i = const.tile([P, N_TOK], I32, name="whole_i")
+            whole_f = const.tile([P, N_TOK], F32, name="whole_f")
+            nc.vector.tensor_scalar(out=turns[:], in0=n_iota[:], scalar1=fcol[:, 0:1], scalar2=None, op0=ALU.mult)
+            nc.vector.tensor_copy(out=whole_i[:], in_=turns[:])
+            nc.vector.tensor_copy(out=whole_f[:], in_=whole_i[:])
+            nc.vector.tensor_tensor(out=turns[:], in0=turns[:], in1=whole_f[:], op=ALU.subtract)
+            nc.scalar.activation(out=sin_t[:], in_=turns[:], func=ACT.Sin, scale=2.0 * math.pi)
+            nc.scalar.activation(out=whole_f[:], in_=turns[:], func=ACT.Abs)
+            nc.gpsimd.tensor_scalar(out=whole_f[:], in0=whole_f[:], scalar1=-1.0, scalar2=0.25,
+                                    op0=ALU.mult, op1=ALU.add)
+            nc.scalar.activation(out=cos_t[:], in_=whole_f[:], func=ACT.Sin, scale=2.0 * math.pi)
+            nc.vector.tensor_copy(out=b_f[:], in_=b_raw[:])
+
+        accs = {}
+        rot = {}
+        ots = {}
+
+        def mx(t):
+            h, s = t // 2, t % 2
+            cod, sca = w_codes[h]
+            for e in range(2):
+                accs[(t, e)] = acc_pool.tile([P, HALF], F32, name="acc", tag="acc")
+            if t == 0:
+                order = [(g, e) for g in range(G) for e in range(2)]
+            else:
+                order = [(g, e) for e in range(2) for g in range(G)]
+            for g, e in order:
+                nc.tensor.matmul_mx(
+                    out=accs[(t, e)][:],
+                    lhsT=cod[:, g, P * e:P * (e + 1)].bitcast(E4X4),
+                    lhsT_scale=sca[:, g, P * e:P * (e + 1)],
+                    rhs=xc[s][:, g, :].bitcast(E5X4),
+                    rhs_scale=xs[s][:, g, :],
+                    start=(g == 0), stop=(g == G - 1))
+
+        def epilogue(t):
+            h, s = t // 2, t % 2
+            cs = cos_t[:, HALF * s:HALF * (s + 1)]
+            sn = sin_t[:, HALF * s:HALF * (s + 1)]
+            ec = ep3.tile([P, HALF], F32, name="ec", tag="ec")
+            oc = ep3.tile([P, HALF], F32, name="oc", tag="oc")
+            es = ep2.tile([P, HALF], F32, name="es", tag="es")
+            os_ = ep2.tile([P, HALF], F32, name="os_", tag="os_")
+            be = b_f[:, h, 0:1]
+            bo = b_f[:, h, 1:2]
+            nc.vector.scalar_tensor_tensor(out=ec[:], in0=accs[(t, 0)][:], scalar=be, in1=cs, op0=ALU.add, op1=ALU.mult)
+            nc.vector.scalar_tensor_tensor(out=es[:], in0=accs[(t, 0)][:], scalar=be, in1=sn, op0=ALU.add, op1=ALU.mult)
+            nc.vector.scalar_tensor_tensor(out=os_[:], in0=accs[(t, 1)][:], scalar=bo, in1=sn, op0=ALU.add, op1=ALU.mult)
+            nc.vector.scalar_tensor_tensor(out=oc[:], in0=accs[(t, 1)][:], scalar=bo, in1=cs, op0=ALU.add, op1=ALU.mult)
+            eng = nc.gpsimd if ADD_ON_GPSIMD else nc.vector
+            eng.tensor_tensor(out=ec[:], in0=ec[:], in1=os_[:], op=ALU.subtract)
+            eng.tensor_tensor(out=oc[:], in0=oc[:], in1=es[:], op=ALU.add)
+            rot[t] = (ec, oc)
+
+        def out_transposes(t):
+            ec, oc = rot[t]
+            for a in range(2):
+                ot = tp_pool.tile([P, 2, 2, P], F32, name="ot", tag="tp")
+                for ii in range(2):
+                    i = 2 * a + ii
+                    nc.tensor.transpose(ot[:, ii, 0, :], ec[:, P * i:P * (i + 1)], ident[:])
+                    nc.tensor.transpose(ot[:, ii, 1, :], oc[:, P * i:P * (i + 1)], ident[:])
+                ots[(t, a)] = ot
+
+        def out_store(t):
+            h, s = t // 2, t % 2
+            res = ep3.tile([P, 4, D], F32, name="res", tag="res")
+            for a in range(2):
+                dst = res[:, 2 * a:2 * a + 2, :].rearrange("p i (j e) -> p i j e", e=2)
+                src = ots[(t, a)][:].rearrange("p i e j -> p i j e")
+                nc.scalar.copy(out=dst, in_=src)
+            nc.sync.dma_start(
+                out=out[0, h, HALF * s:HALF * (s + 1), :].rearrange("(r i) d -> r (i d)", i=4),
+                in_=res[:].rearrange("p i d -> p (i d)"))
+
+        tables()
+        ctx.enter_context(tc.manual_schedule(engines={mybir.EngineType.PE}))
+        w_tiles(0)
+        for g in range(G):
+            x_prep(0, g)
+            w_interleave(0, g, "v")
+            x_quant(0, g)
+            w_quant1(0, g)
+        w_tiles(1)
+        for g in range(G):
+            w_interleave(1, g, "v")
+
+        units = 2 * H
+        for t in range(units + 2):
+            if t < units:
+                mx(t)
+            if t == 0:
+                for g in range(G):
+                    x_prep(1, g)
+                    x_quant(1, g)
+                for a in range(2):
+                    w_quant2(1, a)
+            if t >= 2:
+                out_transposes(t - 2)
+            if t < units:
+                epilogue(t)
+            if t >= 2:
+                out_store(t - 2)
+            hh, part = (t + 4) // 2, t % 2
+            if hh < H:
+                if part == 0:
+                    w_tiles(hh)
+                for g in (2 * part, 2 * part + 1):
+                    w_interleave(hh, g, "s")
+                w_quant2(hh, part)

@@ -21,7 +21,6 @@ P = 128
 G = 4
 HALF = 512
 CHUNKS = ((0, 1), (1, 1), (2, 2), (4, 2), (6, 2))
-ADD_ON_GPSIMD = True
 
 
 def tile_multiscaleretention_pa_kernel(tc, x, w, b, out):
@@ -187,7 +186,7 @@ def tile_multiscaleretention_pa_kernel(tc, x, w, b, out):
             sn = sin_t[:, HALF * s:HALF * (s + 1)]
             ec = ep3.tile([P, HALF], F32, name="ec", tag="ec")
             oc = ep3.tile([P, HALF], F32, name="oc", tag="oc")
-            es = ep2.tile([P, HALF], F32, name="es", tag="es")
+            es = ep3.tile([P, HALF], F32, name="es", tag="es")
             os_ = ep2.tile([P, HALF], F32, name="os_", tag="os_")
             be = b_f[:, h, 0:1]
             bo = b_f[:, h, 1:2]
@@ -195,19 +194,20 @@ def tile_multiscaleretention_pa_kernel(tc, x, w, b, out):
             nc.vector.scalar_tensor_tensor(out=es[:], in0=accs[(t, 0)][:], scalar=be, in1=sn, op0=ALU.add, op1=ALU.mult)
             nc.vector.scalar_tensor_tensor(out=os_[:], in0=accs[(t, 1)][:], scalar=bo, in1=sn, op0=ALU.add, op1=ALU.mult)
             nc.vector.scalar_tensor_tensor(out=oc[:], in0=accs[(t, 1)][:], scalar=bo, in1=cs, op0=ALU.add, op1=ALU.mult)
-            eng = nc.gpsimd if ADD_ON_GPSIMD else nc.vector
-            eng.tensor_tensor(out=ec[:], in0=ec[:], in1=os_[:], op=ALU.subtract)
-            eng.tensor_tensor(out=oc[:], in0=oc[:], in1=es[:], op=ALU.add)
-            rot[t] = (ec, oc)
+            nc.vector.tensor_tensor(out=ec[:], in0=ec[:], in1=os_[:], op=ALU.subtract)
+            rot[t] = (ec, oc, es)
 
         def out_transposes(t):
-            ec, oc = rot[t]
+            ec, oc, es = rot[t]
             for a in range(2):
                 ot = tp_pool.tile([P, 2, 2, P], F32, name="ot", tag="tp")
                 for ii in range(2):
                     i = 2 * a + ii
                     nc.tensor.transpose(ot[:, ii, 0, :], ec[:, P * i:P * (i + 1)], ident[:])
-                    nc.tensor.transpose(ot[:, ii, 1, :], oc[:, P * i:P * (i + 1)], ident[:])
+                    nc.tensor.matmul(ot[:, ii, 1, :], lhsT=oc[:, P * i:P * (i + 1)], rhs=ident[:],
+                                     is_transpose=True, start=True, stop=False)
+                    nc.tensor.matmul(ot[:, ii, 1, :], lhsT=es[:, P * i:P * (i + 1)], rhs=ident[:],
+                                     is_transpose=True, start=False, stop=True)
                 ots[(t, a)] = ot
 
         def out_store(t):

@@ -20,7 +20,8 @@ ACT = mybir.ActivationFunctionType
 P = 128
 G = 4
 HALF = 512
-CHUNKS = ((0, 1), (1, 1), (2, 2), (4, 2), (6, 2))
+CHUNKS = ((0, 1), (1, 1), (2, 2), (4, 4))
+UNITS = ((0, 0), (1, 0), (0, 1), (1, 1)) + tuple((h, s) for h in range(2, H) for s in range(2))
 
 
 def tile_multiscaleretention_pa_kernel(tc, x, w, b, out):
@@ -64,14 +65,17 @@ def tile_multiscaleretention_pa_kernel(tc, x, w, b, out):
             for hl in range(nh):
                 head_src[(h0 + hl, g)] = t[:, :, D * hl:D * (hl + 1)]
 
-        b_raw = const.tile([P, H, 2], BF16, name="b_raw")
+        b_rows = const.tile([P, 2 * P], BF16, name="b_rows")
+        nc.vector.memset(b_rows[:], 0.0)
         for g in range(G):
             load_x(0, g)
             load_w(0, g)
-        nc.sync.dma_start(out=b_raw[:], in_=b.rearrange("(h j e) -> j h e", h=H, e=2))
+        nc.sync.dma_start(out=b_rows[0:H, :], in_=b.rearrange("(h c) -> h c", h=H))
+        for g in range(G):
+            load_w(1, g)
         for g in range(G):
             load_x(1, g)
-        for c in range(1, len(CHUNKS)):
+        for c in range(2, len(CHUNKS)):
             for g in range(G):
                 load_w(c, g)
 
@@ -156,21 +160,27 @@ def tile_multiscaleretention_pa_kernel(tc, x, w, b, out):
             nc.gpsimd.tensor_scalar(out=whole_f[:], in0=whole_f[:], scalar1=-1.0, scalar2=0.25,
                                     op0=ALU.mult, op1=ALU.add)
             nc.scalar.activation(out=cos_t[:], in_=whole_f[:], func=ACT.Sin, scale=2.0 * math.pi)
-            nc.vector.tensor_copy(out=b_f[:], in_=b_raw[:])
+
+        def bias_columns():
+            bt = tp_pool.tile([P, 2, 2, P], F32, name="bt", tag="tp")
+            nc.tensor.transpose(bt[:, 0, 0, :], b_rows[:].bitcast(F32), ident[:])
+            b_w = const.tile([P, H], F32, name="b_w")
+            nc.vector.tensor_copy(out=b_w[:], in_=bt[:, 0, 0, 0:H])
+            nc.vector.tensor_copy(out=b_f[:].rearrange("p h e -> p (h e)"), in_=b_w[:].bitcast(BF16))
 
         accs = {}
         rot = {}
         ots = {}
 
-        def mx(t):
-            h, s = t // 2, t % 2
+        def mx(t, banks):
+            h, s = UNITS[t]
             cod, sca = w_codes[h]
-            for e in range(2):
+            for e in banks:
                 accs[(t, e)] = acc_pool.tile([P, HALF], F32, name="acc", tag="acc")
-            if t == 0:
-                order = [(g, e) for g in range(G) for e in range(2)]
+            if len(banks) == 2:
+                order = [(g, e) for g in range(G) for e in banks]
             else:
-                order = [(g, e) for e in range(2) for g in range(G)]
+                order = [(g, e) for e in banks for g in range(G)]
             for g, e in order:
                 nc.tensor.matmul_mx(
                     out=accs[(t, e)][:],
@@ -180,79 +190,118 @@ def tile_multiscaleretention_pa_kernel(tc, x, w, b, out):
                     rhs_scale=xs[s][:, g, :],
                     start=(g == 0), stop=(g == G - 1))
 
-        def epilogue(t):
-            h, s = t // 2, t % 2
-            cs = cos_t[:, HALF * s:HALF * (s + 1)]
-            sn = sin_t[:, HALF * s:HALF * (s + 1)]
+        def epi_even_bank(t):
+            h, s = UNITS[t]
             ec = ep3.tile([P, HALF], F32, name="ec", tag="ec")
-            oc = ep3.tile([P, HALF], F32, name="oc", tag="oc")
             es = ep3.tile([P, HALF], F32, name="es", tag="es")
-            os_ = ep2.tile([P, HALF], F32, name="os_", tag="os_")
             be = b_f[:, h, 0:1]
-            bo = b_f[:, h, 1:2]
-            nc.vector.scalar_tensor_tensor(out=ec[:], in0=accs[(t, 0)][:], scalar=be, in1=cs, op0=ALU.add, op1=ALU.mult)
-            nc.vector.scalar_tensor_tensor(out=es[:], in0=accs[(t, 0)][:], scalar=be, in1=sn, op0=ALU.add, op1=ALU.mult)
-            nc.vector.scalar_tensor_tensor(out=os_[:], in0=accs[(t, 1)][:], scalar=bo, in1=sn, op0=ALU.add, op1=ALU.mult)
-            nc.vector.scalar_tensor_tensor(out=oc[:], in0=accs[(t, 1)][:], scalar=bo, in1=cs, op0=ALU.add, op1=ALU.mult)
-            nc.vector.tensor_tensor(out=ec[:], in0=ec[:], in1=os_[:], op=ALU.subtract)
-            rot[t] = (ec, oc, es)
+            nc.vector.scalar_tensor_tensor(out=ec[:], in0=accs[(t, 0)][:], scalar=be,
+                                           in1=cos_t[:, HALF * s:HALF * (s + 1)], op0=ALU.add, op1=ALU.mult)
+            nc.vector.scalar_tensor_tensor(out=es[:], in0=accs[(t, 0)][:], scalar=be,
+                                           in1=sin_t[:, HALF * s:HALF * (s + 1)], op0=ALU.add, op1=ALU.mult)
+            rot[t] = [ec, es]
 
-        def out_transposes(t):
-            ec, oc, es = rot[t]
-            for a in range(2):
-                ot = tp_pool.tile([P, 2, 2, P], F32, name="ot", tag="tp")
-                for ii in range(2):
-                    i = 2 * a + ii
-                    nc.tensor.transpose(ot[:, ii, 0, :], ec[:, P * i:P * (i + 1)], ident[:])
-                    nc.tensor.matmul(ot[:, ii, 1, :], lhsT=oc[:, P * i:P * (i + 1)], rhs=ident[:],
-                                     is_transpose=True, start=True, stop=False)
-                    nc.tensor.matmul(ot[:, ii, 1, :], lhsT=es[:, P * i:P * (i + 1)], rhs=ident[:],
-                                     is_transpose=True, start=False, stop=True)
-                ots[(t, a)] = ot
+        def epi_odd_bank(t):
+            h, s = UNITS[t]
+            os_ = ep2.tile([P, HALF], F32, name="os_", tag="os_")
+            oc = ep3.tile([P, HALF], F32, name="oc", tag="oc")
+            bo = b_f[:, h, 1:2]
+            nc.vector.scalar_tensor_tensor(out=os_[:], in0=accs[(t, 1)][:], scalar=bo,
+                                           in1=sin_t[:, HALF * s:HALF * (s + 1)], op0=ALU.add, op1=ALU.mult)
+            nc.vector.scalar_tensor_tensor(out=oc[:], in0=accs[(t, 1)][:], scalar=bo,
+                                           in1=cos_t[:, HALF * s:HALF * (s + 1)], op0=ALU.add, op1=ALU.mult)
+            ec = rot[t][0]
+            nc.gpsimd.tensor_tensor(out=ec[:], in0=ec[:], in1=os_[:], op=ALU.subtract)
+            rot[t].append(oc)
+
+        def out_transposes(t, a):
+            ec, es, oc = rot[t]
+            ot = tp_pool.tile([P, 2, 2, P], F32, name="ot", tag="tp")
+            for ii in range(2):
+                i = 2 * a + ii
+                nc.tensor.transpose(ot[:, ii, 0, :], ec[:, P * i:P * (i + 1)], ident[:])
+                nc.tensor.matmul(ot[:, ii, 1, :], lhsT=oc[:, P * i:P * (i + 1)], rhs=ident[:],
+                                 is_transpose=True, start=True, stop=False)
+                nc.tensor.matmul(ot[:, ii, 1, :], lhsT=es[:, P * i:P * (i + 1)], rhs=ident[:],
+                                 is_transpose=True, start=False, stop=True)
+            ots[(t, a)] = ot
+
+        results = {}
+
+        def out_copy(t, a):
+            if a == 0:
+                results[t] = ep3.tile([P, 4, D], F32, name="res", tag="res")
+            nc.scalar.copy(out=results[t][:, 2 * a:2 * a + 2, :].rearrange("p i (j e) -> p i j e", e=2),
+                           in_=ots[(t, a)][:].rearrange("p i e j -> p i j e"))
 
         def out_store(t):
-            h, s = t // 2, t % 2
-            res = ep3.tile([P, 4, D], F32, name="res", tag="res")
-            for a in range(2):
-                dst = res[:, 2 * a:2 * a + 2, :].rearrange("p i (j e) -> p i j e", e=2)
-                src = ots[(t, a)][:].rearrange("p i e j -> p i j e")
-                nc.scalar.copy(out=dst, in_=src)
+            h, s = UNITS[t]
             nc.sync.dma_start(
                 out=out[0, h, HALF * s:HALF * (s + 1), :].rearrange("(r i) d -> r (i d)", i=4),
-                in_=res[:].rearrange("p i d -> p (i d)"))
+                in_=results[t][:].rearrange("p i d -> p (i d)"))
 
         tables()
-        ctx.enter_context(tc.manual_schedule(engines={mybir.EngineType.PE}))
         w_tiles(0)
         for g in range(G):
             x_prep(0, g)
             w_interleave(0, g, "v")
             x_quant(0, g)
             w_quant1(0, g)
-        w_tiles(1)
-        for g in range(G):
-            w_interleave(1, g, "v")
+        bias_columns()
 
-        units = 2 * H
+        ctx.enter_context(tc.manual_schedule())
+        w_tiles(1)
+        w_interleave(1, 0, "s")
+        w_interleave(1, 1, "s")
+        w_interleave(1, 2, "v")
+        w_interleave(1, 3, "v")
+        units = len(UNITS)
+        pending = [(1, 0), (1, 1)]
         for t in range(units + 2):
-            if t < units:
-                mx(t)
+            hh, part = (t + 3) // 2, (t + 1) % 2
+            prep = 2 <= hh < H
             if t == 0:
-                for g in range(G):
-                    x_prep(1, g)
-                    x_quant(1, g)
-                for a in range(2):
-                    w_quant2(1, a)
+                mx(0, (0, 1))
+            elif t < units:
+                mx(t, (0,))
+            if t == 1:
+                x_prep(1, 0)
+                x_prep(1, 1)
             if t >= 2:
-                out_transposes(t - 2)
+                out_transposes(t - 2, 0)
+            if t == 0:
+                for hq, aq in pending:
+                    w_quant2(hq, aq)
+                pending = []
             if t < units:
-                epilogue(t)
+                epi_even_bank(t)
             if t >= 2:
-                out_store(t - 2)
-            hh, part = (t + 4) // 2, t % 2
-            if hh < H:
+                out_copy(t - 2, 0)
+            for hq, aq in pending:
+                w_quant2(hq, aq)
+            pending = []
+            if t == 1:
+                x_quant(1, 0)
+                x_quant(1, 1)
+            if prep:
                 if part == 0:
                     w_tiles(hh)
-                for g in (2 * part, 2 * part + 1):
-                    w_interleave(hh, g, "s")
-                w_quant2(hh, part)
+                w_interleave(hh, 2 * part, "s")
+            if 0 < t < units:
+                mx(t, (1,))
+            if t == 1:
+                x_prep(1, 2)
+                x_prep(1, 3)
+            if t >= 2:
+                out_transposes(t - 2, 1)
+            if t < units:
+                epi_odd_bank(t)
+            if t == 1:
+                x_quant(1, 2)
+                x_quant(1, 3)
+            if t >= 2:
+                out_copy(t - 2, 1)
+                out_store(t - 2)
+            if prep:
+                w_interleave(hh, 2 * part + 1, "s")
+                pending.append((hh, part))

@@ -123,6 +123,10 @@ def tile_multiscaleretention_pa_kernel(tc, x, w, b, out):
             src = head_src[(h, g)].rearrange("p t (j e) -> p e j t", e=2)
             if eng == "s":
                 nc.scalar.copy(out=dst, in_=src)
+            elif eng == "g":
+                for e in range(2):
+                    nc.gpsimd.tensor_scalar(out=dst[:, e], in0=src[:, e], scalar1=1.0, scalar2=0.0,
+                                            op0=ALU.mult, op1=ALU.add)
             else:
                 nc.vector.tensor_copy(out=dst, in_=src)
 
@@ -287,6 +291,7 @@ def tile_multiscaleretention_pa_kernel(tc, x, w, b, out):
                 if part == 0:
                     w_tiles(hh)
                 w_interleave(hh, 2 * part, "s")
+                w_interleave(hh, 2 * part + 1, "g")
             if 0 < t < units:
                 mx(t, (1,))
             if t == 1:
@@ -303,5 +308,4 @@ def tile_multiscaleretention_pa_kernel(tc, x, w, b, out):
                 out_copy(t - 2, 1)
                 out_store(t - 2)
             if prep:
-                w_interleave(hh, 2 * part + 1, "s")
                 pending.append((hh, part))

@@ -20,7 +20,7 @@ ACT = mybir.ActivationFunctionType
 P = 128
 G = 4
 HALF = 512
-CHUNKS = ((0, 1), (1, 1), (2, 2), (4, 4))
+CHUNKS = ((0, 2), (2, 2), (4, 4))
 UNITS = ((0, 0), (1, 0), (0, 1), (1, 1)) + tuple((h, s) for h in range(2, H) for s in range(2))
 
 
@@ -46,15 +46,15 @@ def tile_multiscaleretention_pa_kernel(tc, x, w, b, out):
         nc.gpsimd.iota(n_iota[:], pattern=[[HALF, 2], [1, 4], [4, P]], base=0,
                        channel_multiplier=0, allow_small_or_imprecise_dtypes=True)
 
-        xv = x[0].rearrange("(s r i) k -> s r i k", s=2, i=4)
+        xv = x[0].rearrange("(s r a i) k -> s a r i k", s=2, a=2, i=2)
         x_raw = {}
         w_raw = {}
         head_src = {}
 
-        def load_x(s, g):
-            t = const.tile([P, 4, 512], BF16, name="x_raw%d%d" % (s, g))
-            nc.sync.dma_start(out=t[:], in_=xv[s, :, :, 512 * g:512 * (g + 1)])
-            x_raw[(s, g)] = t
+        def load_x(s, a):
+            t = const.tile([P, 2, E], BF16, name="x_raw%d%d" % (s, a))
+            nc.sync.dma_start(out=t[:], in_=xv[s, a])
+            x_raw[(s, a)] = t
 
         def load_w(c, g):
             h0, nh = CHUNKS[c]
@@ -67,15 +67,14 @@ def tile_multiscaleretention_pa_kernel(tc, x, w, b, out):
 
         b_rows = const.tile([P, 2 * P], BF16, name="b_rows")
         nc.vector.memset(b_rows[:], 0.0)
+        load_x(0, 0)
+        load_x(0, 1)
         for g in range(G):
-            load_x(0, g)
             load_w(0, g)
         nc.sync.dma_start(out=b_rows[0:H, :], in_=b.rearrange("(h c) -> h c", h=H))
-        for g in range(G):
-            load_w(1, g)
-        for g in range(G):
-            load_x(1, g)
-        for c in range(2, len(CHUNKS)):
+        load_x(1, 0)
+        load_x(1, 1)
+        for c in range(1, len(CHUNKS)):
             for g in range(G):
                 load_w(c, g)
 
@@ -98,16 +97,16 @@ def tile_multiscaleretention_pa_kernel(tc, x, w, b, out):
         xc = [const.tile([P, G, HALF], U32, name="xc%d" % s, align_bytes=64) for s in range(2)]
         xs = [const.tile([P, G, HALF], U8, name="xs%d" % s, align_bytes=64) for s in range(2)]
 
-        def x_prep(s, g):
-            words = x_raw[(s, g)][:].bitcast(F32)
+        def x_prep(s, i):
+            words = x_raw[(s, i // 2)][:, i % 2, :].bitcast(F32)
             for a in range(2):
                 xt = tp_pool.tile([P, 2, 2, P], F32, name="xt", tag="tp")
-                for ii in range(2):
+                for gg in range(2):
+                    g = 2 * a + gg
                     for u in range(2):
-                        nc.tensor.transpose(xt[:, ii, u, :], words[:, 2 * a + ii, u:256:2], ident[:])
-                dst = xg_w[:, g, 256 * a:256 * (a + 1), :].rearrange("p (i r) u -> p i r u", i=2)
-                src = xt[:].rearrange("p i u r -> p i r u")
-                nc.scalar.copy(out=dst, in_=src)
+                        nc.tensor.transpose(xt[:, gg, u, :], words[:, 256 * g + u:256 * (g + 1):2], ident[:])
+                nc.scalar.copy(out=xg_w[:, 2 * a:2 * a + 2, P * i:P * (i + 1), :],
+                               in_=xt[:].rearrange("p g u r -> p g r u"))
 
         def x_quant(s, g):
             nc.vector.quantize_mx(out=xc[s][:, g, :].bitcast(E5X4), scales=xs[s][:, g, :], in_=xg[:, g, :])
@@ -123,10 +122,6 @@ def tile_multiscaleretention_pa_kernel(tc, x, w, b, out):
             src = head_src[(h, g)].rearrange("p t (j e) -> p e j t", e=2)
             if eng == "s":
                 nc.scalar.copy(out=dst, in_=src)
-            elif eng == "g":
-                for e in range(2):
-                    nc.gpsimd.tensor_scalar(out=dst[:, e], in0=src[:, e], scalar1=1.0, scalar2=0.0,
-                                            op0=ALU.mult, op1=ALU.add)
             else:
                 nc.vector.tensor_copy(out=dst, in_=src)
 
@@ -246,8 +241,9 @@ def tile_multiscaleretention_pa_kernel(tc, x, w, b, out):
 
         tables()
         w_tiles(0)
+        for i in range(4):
+            x_prep(0, i)
         for g in range(G):
-            x_prep(0, g)
             w_interleave(0, g, "v")
             x_quant(0, g)
             w_quant1(0, g)
@@ -284,14 +280,10 @@ def tile_multiscaleretention_pa_kernel(tc, x, w, b, out):
             for hq, aq in pending:
                 w_quant2(hq, aq)
             pending = []
-            if t == 1:
-                x_quant(1, 0)
-                x_quant(1, 1)
             if prep:
                 if part == 0:
                     w_tiles(hh)
                 w_interleave(hh, 2 * part, "s")
-                w_interleave(hh, 2 * part + 1, "g")
             if 0 < t < units:
                 mx(t, (1,))
             if t == 1:
@@ -302,10 +294,11 @@ def tile_multiscaleretention_pa_kernel(tc, x, w, b, out):
             if t < units:
                 epi_odd_bank(t)
             if t == 1:
-                x_quant(1, 2)
-                x_quant(1, 3)
+                for g in range(G):
+                    x_quant(1, g)
             if t >= 2:
                 out_copy(t - 2, 1)
                 out_store(t - 2)
             if prep:
+                w_interleave(hh, 2 * part + 1, "s")
                 pending.append((hh, part))

@@ -20,8 +20,11 @@ ACT = mybir.ActivationFunctionType
 P = 128
 G = 4
 HALF = 512
-CHUNKS = ((0, 2), (2, 2), (4, 4))
+CHUNKS = ((0, 1), (1, 1), (2, 2), (4, 4))
 UNITS = ((0, 0), (1, 0), (0, 1), (1, 1)) + tuple((h, s) for h in range(2, H) for s in range(2))
+WI_ENGINE = "sssv"
+LEAD = 4
+SPLIT = True
 
 
 def tile_multiscaleretention_pa_kernel(tc, x, w, b, out):
@@ -34,9 +37,11 @@ def tile_multiscaleretention_pa_kernel(tc, x, w, b, out):
         ep2 = ctx.enter_context(tc.tile_pool(name="ep2", bufs=2))
         acc_pool = ctx.enter_context(tc.psum_pool(name="acc", bufs=4))
         tp_pool = ctx.enter_context(tc.psum_pool(name="tp", bufs=4))
+        ctx.enter_context(tc.manual_schedule())
 
         ones = const.tile([P, 1], F32, name="ones")
         nc.vector.memset(ones[:], 1.0)
+        b_bf = const.tile([P, H, 2], BF16, name="b_bf")
         scr = const.tile([P, 1], F32, name="scr")
         nc.scalar.activation(out=scr[:], in_=ones[:], func=ACT.Sin, scale=1.0)
 
@@ -46,15 +51,14 @@ def tile_multiscaleretention_pa_kernel(tc, x, w, b, out):
         nc.gpsimd.iota(n_iota[:], pattern=[[HALF, 2], [1, 4], [4, P]], base=0,
                        channel_multiplier=0, allow_small_or_imprecise_dtypes=True)
 
-        xv = x[0].rearrange("(s r a i) k -> s a r i k", s=2, a=2, i=2)
+        xv = x[0].rearrange("(s r i) (g k) -> s g r i k", s=2, i=4, g=G)
         x_raw = {}
-        w_raw = {}
         head_src = {}
 
-        def load_x(s, a):
-            t = const.tile([P, 2, E], BF16, name="x_raw%d%d" % (s, a))
-            nc.sync.dma_start(out=t[:], in_=xv[s, a])
-            x_raw[(s, a)] = t
+        def load_x(s, g):
+            t = const.tile([P, 4, 512], BF16, name="x_raw%d%d" % (s, g))
+            nc.sync.dma_start(out=t[:], in_=xv[s, g])
+            x_raw[(s, g)] = t
 
         def load_w(c, g):
             h0, nh = CHUNKS[c]
@@ -65,16 +69,17 @@ def tile_multiscaleretention_pa_kernel(tc, x, w, b, out):
             for hl in range(nh):
                 head_src[(h0 + hl, g)] = t[:, :, D * hl:D * (hl + 1)]
 
-        b_rows = const.tile([P, 2 * P], BF16, name="b_rows")
-        nc.vector.memset(b_rows[:], 0.0)
         load_x(0, 0)
-        load_x(0, 1)
-        for g in range(G):
+        load_w(0, 0)
+        nc.sync.dma_start(out=b_bf[:], in_=b.rearrange("(h j e) -> j h e", h=H, e=2))
+        for g in range(1, G):
+            load_x(0, g)
             load_w(0, g)
-        nc.sync.dma_start(out=b_rows[0:H, :], in_=b.rearrange("(h c) -> h c", h=H))
-        load_x(1, 0)
-        load_x(1, 1)
-        for c in range(1, len(CHUNKS)):
+        for g in range(G):
+            load_w(1, g)
+        for g in range(G):
+            load_x(1, g)
+        for c in range(2, len(CHUNKS)):
             for g in range(G):
                 load_w(c, g)
 
@@ -93,20 +98,24 @@ def tile_multiscaleretention_pa_kernel(tc, x, w, b, out):
         nc.vector.tensor_reduce(out=fcol[:], in_=fdiag[:], axis=mybir.AxisListType.X, op=ALU.add)
 
         xg = const.tile([P, G, 4 * HALF], BF16, name="xg", align_bytes=64)
-        xg_w = xg[:].bitcast(F32).rearrange("p g (c u) -> p g c u", u=2)
+        xg_w = xg[:].bitcast(F32).rearrange("p g (i r u) -> p g i r u", i=4, u=2)
         xc = [const.tile([P, G, HALF], U32, name="xc%d" % s, align_bytes=64) for s in range(2)]
         xs = [const.tile([P, G, HALF], U8, name="xs%d" % s, align_bytes=64) for s in range(2)]
+        xts = {}
 
-        def x_prep(s, i):
-            words = x_raw[(s, i // 2)][:, i % 2, :].bitcast(F32)
+        def x_transposes(s, g):
             for a in range(2):
                 xt = tp_pool.tile([P, 2, 2, P], F32, name="xt", tag="tp")
-                for gg in range(2):
-                    g = 2 * a + gg
+                for ii in range(2):
+                    words = x_raw[(s, g)][:, 2 * a + ii, :].bitcast(F32)
                     for u in range(2):
-                        nc.tensor.transpose(xt[:, gg, u, :], words[:, 256 * g + u:256 * (g + 1):2], ident[:])
-                nc.scalar.copy(out=xg_w[:, 2 * a:2 * a + 2, P * i:P * (i + 1), :],
-                               in_=xt[:].rearrange("p g u r -> p g r u"))
+                        nc.tensor.transpose(xt[:, ii, u, :], words[:, u:256:2], ident[:])
+                xts[(s, g, a)] = xt
+
+        def x_copies(s, g):
+            for a in range(2):
+                nc.scalar.copy(out=xg_w[:, g, 2 * a:2 * a + 2, :, :],
+                               in_=xts[(s, g, a)][:].rearrange("p i u r -> p i r u"))
 
         def x_quant(s, g):
             nc.vector.quantize_mx(out=xc[s][:, g, :].bitcast(E5X4), scales=xs[s][:, g, :], in_=xg[:, g, :])
@@ -115,15 +124,19 @@ def tile_multiscaleretention_pa_kernel(tc, x, w, b, out):
         wg_tiles = {}
 
         def w_interleave(h, g, eng):
-            if g % 2 == 0:
+            if (h, g // 2) not in wg_tiles:
                 wg_tiles[(h, g // 2)] = wg_pool.tile([P, 2, 4 * D], BF16, name="wg", tag="wg", align_bytes=64)
             t = wg_tiles[(h, g // 2)]
             dst = t[:, g % 2, :].rearrange("p (e j t) -> p e j t", e=2, t=4)
             src = head_src[(h, g)].rearrange("p t (j e) -> p e j t", e=2)
             if eng == "s":
                 nc.scalar.copy(out=dst, in_=src)
-            else:
+            elif eng == "v":
                 nc.vector.tensor_copy(out=dst, in_=src)
+            else:
+                for e in range(2):
+                    nc.gpsimd.tensor_scalar(out=dst[:, e], in0=src[:, e], scalar1=1.0, scalar2=0.0,
+                                            op0=ALU.mult, op1=ALU.add)
 
         def w_tiles(h):
             cod = wc_pool.tile([P, G, D], U32, name="wcod", tag="wcod", align_bytes=64)
@@ -144,50 +157,58 @@ def tile_multiscaleretention_pa_kernel(tc, x, w, b, out):
 
         cos_t = const.tile([P, N_TOK], F32, name="cos_t")
         sin_t = const.tile([P, N_TOK], F32, name="sin_t")
+        turns = const.tile([P, N_TOK], F32, name="turns")
+        whole_i = const.tile([P, N_TOK], I32, name="whole_i")
+        whole_f = const.tile([P, N_TOK], F32, name="whole_f")
         b_f = const.tile([P, H, 2], F32, name="b_f")
 
-        def tables():
-            turns = const.tile([P, N_TOK], F32, name="turns")
-            whole_i = const.tile([P, N_TOK], I32, name="whole_i")
-            whole_f = const.tile([P, N_TOK], F32, name="whole_f")
-            nc.vector.tensor_scalar(out=turns[:], in0=n_iota[:], scalar1=fcol[:, 0:1], scalar2=None, op0=ALU.mult)
-            nc.vector.tensor_copy(out=whole_i[:], in_=turns[:])
-            nc.vector.tensor_copy(out=whole_f[:], in_=whole_i[:])
-            nc.vector.tensor_tensor(out=turns[:], in0=turns[:], in1=whole_f[:], op=ALU.subtract)
-            nc.scalar.activation(out=sin_t[:], in_=turns[:], func=ACT.Sin, scale=2.0 * math.pi)
-            nc.scalar.activation(out=whole_f[:], in_=turns[:], func=ACT.Abs)
-            nc.gpsimd.tensor_scalar(out=whole_f[:], in0=whole_f[:], scalar1=-1.0, scalar2=0.25,
+        def tables_vector(s):
+            c = slice(HALF * s, HALF * (s + 1))
+            nc.vector.tensor_scalar(out=whole_i[:, c], in0=n_iota[:, c], scalar1=fcol[:, 0:1], scalar2=None, op0=ALU.mult)
+            nc.vector.scalar_tensor_tensor(out=turns[:, c], in0=n_iota[:, c], scalar=fcol[:, 0:1], in1=whole_i[:, c],
+                                           op0=ALU.mult, op1=ALU.subtract)
+
+        def tables_sin(s):
+            c = slice(HALF * s, HALF * (s + 1))
+            nc.scalar.activation(out=sin_t[:, c], in_=turns[:, c], func=ACT.Sin, scale=2.0 * math.pi)
+
+        def tables_abs(s):
+            c = slice(HALF * s, HALF * (s + 1))
+            nc.scalar.activation(out=whole_f[:, c], in_=turns[:, c], func=ACT.Abs)
+            nc.gpsimd.tensor_scalar(out=whole_f[:, c], in0=whole_f[:, c], scalar1=-1.0, scalar2=0.25,
                                     op0=ALU.mult, op1=ALU.add)
-            nc.scalar.activation(out=cos_t[:], in_=whole_f[:], func=ACT.Sin, scale=2.0 * math.pi)
+
+        def tables_cos(s):
+            c = slice(HALF * s, HALF * (s + 1))
+            nc.scalar.activation(out=cos_t[:, c], in_=whole_f[:, c], func=ACT.Sin, scale=2.0 * math.pi)
 
         def bias_columns():
-            bt = tp_pool.tile([P, 2, 2, P], F32, name="bt", tag="tp")
-            nc.tensor.transpose(bt[:, 0, 0, :], b_rows[:].bitcast(F32), ident[:])
-            b_w = const.tile([P, H], F32, name="b_w")
-            nc.vector.tensor_copy(out=b_w[:], in_=bt[:, 0, 0, 0:H])
-            nc.vector.tensor_copy(out=b_f[:].rearrange("p h e -> p (h e)"), in_=b_w[:].bitcast(BF16))
+            nc.vector.tensor_copy(out=b_f[:], in_=b_bf[:])
 
         accs = {}
         rot = {}
         ots = {}
 
-        def mx(t, banks):
+        def mx_one(t, e, g):
             h, s = UNITS[t]
             cod, sca = w_codes[h]
-            for e in banks:
+            if g == 0:
                 accs[(t, e)] = acc_pool.tile([P, HALF], F32, name="acc", tag="acc")
-            if len(banks) == 2:
-                order = [(g, e) for g in range(G) for e in banks]
-            else:
-                order = [(g, e) for e in banks for g in range(G)]
-            for g, e in order:
-                nc.tensor.matmul_mx(
-                    out=accs[(t, e)][:],
-                    lhsT=cod[:, g, P * e:P * (e + 1)].bitcast(E4X4),
-                    lhsT_scale=sca[:, g, P * e:P * (e + 1)],
-                    rhs=xc[s][:, g, :].bitcast(E5X4),
-                    rhs_scale=xs[s][:, g, :],
-                    start=(g == 0), stop=(g == G - 1))
+            nc.tensor.matmul_mx(
+                out=accs[(t, e)][:],
+                lhsT=cod[:, g, P * e:P * (e + 1)].bitcast(E4X4),
+                lhsT_scale=sca[:, g, P * e:P * (e + 1)],
+                rhs=xc[s][:, g, :].bitcast(E5X4),
+                rhs_scale=xs[s][:, g, :],
+                start=(g == 0), stop=(g == G - 1))
+
+        def mx_pass(t, g):
+            for e in range(2):
+                mx_one(t, e, g)
+
+        def mx_bank(t, e):
+            for g in range(G):
+                mx_one(t, e, g)
 
         def epi_even_bank(t):
             h, s = UNITS[t]
@@ -239,66 +260,101 @@ def tile_multiscaleretention_pa_kernel(tc, x, w, b, out):
                 out=out[0, h, HALF * s:HALF * (s + 1), :].rearrange("(r i) d -> r (i d)", i=4),
                 in_=results[t][:].rearrange("p i d -> p (i d)"))
 
-        tables()
+        tables_vector(0)
         w_tiles(0)
-        for i in range(4):
-            x_prep(0, i)
+        x_transposes(0, 0)
+        x_transposes(0, 1)
         for g in range(G):
+            x_copies(0, g)
+            if g == 0:
+                tables_sin(0)
+            if g == 1:
+                tables_abs(0)
+            if g == 2:
+                tables_cos(0)
+            if g + 2 < G:
+                x_transposes(0, g + 2)
             w_interleave(0, g, "v")
             x_quant(0, g)
             w_quant1(0, g)
+            mx_pass(0, g)
         bias_columns()
-
-        ctx.enter_context(tc.manual_schedule())
         w_tiles(1)
+        x_transposes(1, 0)
+        x_transposes(1, 1)
         w_interleave(1, 0, "s")
-        w_interleave(1, 1, "s")
-        w_interleave(1, 2, "v")
+        w_interleave(1, 1, "v")
+        w_quant1(1, 0)
+        w_interleave(1, 2, "s")
         w_interleave(1, 3, "v")
+        w_quant1(1, 1)
+        mx_pass(1, 0)
+        mx_pass(1, 1)
+        w_quant1(1, 2)
+        w_quant1(1, 3)
+        mx_pass(1, 2)
+        mx_pass(1, 3)
+        epi_even_bank(0)
+        epi_odd_bank(0)
+        tables_vector(1)
+        x_copies(1, 0)
+        x_transposes(1, 2)
+        x_copies(1, 1)
+        x_transposes(1, 3)
+        tables_sin(1)
+        x_quant(1, 0)
+        x_quant(1, 1)
+        epi_even_bank(1)
+        x_copies(1, 2)
+        tables_abs(1)
+        x_copies(1, 3)
+        tables_cos(1)
+        x_quant(1, 2)
+        x_quant(1, 3)
+        epi_odd_bank(1)
         units = len(UNITS)
-        pending = [(1, 0), (1, 1)]
-        for t in range(units + 2):
-            hh, part = (t + 3) // 2, (t + 1) % 2
-            prep = 2 <= hh < H
-            if t == 0:
-                mx(0, (0, 1))
-            elif t < units:
-                mx(t, (0,))
-            if t == 1:
-                x_prep(1, 0)
-                x_prep(1, 1)
-            if t >= 2:
-                out_transposes(t - 2, 0)
-            if t == 0:
-                for hq, aq in pending:
-                    w_quant2(hq, aq)
-                pending = []
-            if t < units:
-                epi_even_bank(t)
-            if t >= 2:
-                out_copy(t - 2, 0)
-            for hq, aq in pending:
-                w_quant2(hq, aq)
-            pending = []
-            if prep:
-                if part == 0:
-                    w_tiles(hh)
-                w_interleave(hh, 2 * part, "s")
-            if 0 < t < units:
-                mx(t, (1,))
-            if t == 1:
-                x_prep(1, 2)
-                x_prep(1, 3)
-            if t >= 2:
+        queue = dict((k, [(h, g) for h in range(2, H) for g in range(G) if WI_ENGINE[g] == k]) for k in "svg")
+        done = set()
+        quantised = set()
+
+        def prep(t, k):
+            if queue[k] and queue[k][0][0] <= (t + LEAD) // 2:
+                h, g = queue[k].pop(0)
+                w_interleave(h, g, k)
+                done.add((h, g))
+
+        def quant_ready():
+            for h in range(2, H):
+                for a in range(2):
+                    if (h, a) not in quantised and (h, 2 * a) in done and (h, 2 * a + 1) in done:
+                        if a == 0:
+                            w_tiles(h)
+                        w_quant2(h, a)
+                        quantised.add((h, a))
+
+        for t in range(2, units + 2):
+            live = t < units
+            if live:
+                mx_bank(t, 0)
+                if not SPLIT:
+                    mx_bank(t, 1)
+            out_transposes(t - 2, 0)
+            if not SPLIT:
                 out_transposes(t - 2, 1)
-            if t < units:
+            quant_ready()
+            if live:
+                epi_even_bank(t)
+            out_copy(t - 2, 0)
+            prep(t, "s")
+            prep(t, "v")
+            prep(t, "g")
+            if live and SPLIT:
+                mx_bank(t, 1)
+            if SPLIT:
+                out_transposes(t - 2, 1)
+            quant_ready()
+            if live:
                 epi_odd_bank(t)
-            if t == 1:
-                for g in range(G):
-                    x_quant(1, g)
-            if t >= 2:
-                out_copy(t - 2, 1)
-                out_store(t - 2)
-            if prep:
-                w_interleave(hh, 2 * part + 1, "s")
-                pending.append((hh, part))
+            out_copy(t - 2, 1)
+            out_store(t - 2)
+            prep(t, "s")

@@ -23,8 +23,9 @@ HALF = 512
 CHUNKS = ((0, 1), (1, 1), (2, 2), (4, 4))
 UNITS = ((0, 0), (1, 0), (0, 1), (1, 1)) + tuple((h, s) for h in range(2, H) for s in range(2))
 WI_ENGINE = "sssv"
+RES_BUFS = 5
 LEAD = 4
-SPLIT = True
+SPLIT = False
 
 
 def tile_multiscaleretention_pa_kernel(tc, x, w, b, out):
@@ -35,6 +36,7 @@ def tile_multiscaleretention_pa_kernel(tc, x, w, b, out):
         wc_pool = ctx.enter_context(tc.tile_pool(name="wc", bufs=3))
         ep3 = ctx.enter_context(tc.tile_pool(name="ep3", bufs=3))
         ep2 = ctx.enter_context(tc.tile_pool(name="ep2", bufs=2))
+        res_pool = ctx.enter_context(tc.tile_pool(name="res", bufs=RES_BUFS))
         acc_pool = ctx.enter_context(tc.psum_pool(name="acc", bufs=4))
         tp_pool = ctx.enter_context(tc.psum_pool(name="tp", bufs=4))
         ctx.enter_context(tc.manual_schedule())
@@ -231,7 +233,7 @@ def tile_multiscaleretention_pa_kernel(tc, x, w, b, out):
             nc.vector.scalar_tensor_tensor(out=oc[:], in0=accs[(t, 1)][:], scalar=bo,
                                            in1=cos_t[:, HALF * s:HALF * (s + 1)], op0=ALU.add, op1=ALU.mult)
             ec = rot[t][0]
-            nc.gpsimd.tensor_tensor(out=ec[:], in0=ec[:], in1=os_[:], op=ALU.subtract)
+            (nc.vector if t == len(UNITS) - 1 else nc.gpsimd).tensor_tensor(out=ec[:], in0=ec[:], in1=os_[:], op=ALU.subtract)
             rot[t].append(oc)
 
         def out_transposes(t, a):
@@ -250,7 +252,7 @@ def tile_multiscaleretention_pa_kernel(tc, x, w, b, out):
 
         def out_copy(t, a):
             if a == 0:
-                results[t] = ep3.tile([P, 4, D], F32, name="res", tag="res")
+                results[t] = res_pool.tile([P, 4, D], F32, name="res", tag="res")
             nc.scalar.copy(out=results[t][:, 2 * a:2 * a + 2, :].rearrange("p i (j e) -> p i j e", e=2),
                            in_=ots[(t, a)][:].rearrange("p i e j -> p i j e"))
 
@@ -259,6 +261,12 @@ def tile_multiscaleretention_pa_kernel(tc, x, w, b, out):
             nc.sync.dma_start(
                 out=out[0, h, HALF * s:HALF * (s + 1), :].rearrange("(r i) d -> r (i d)", i=4),
                 in_=results[t][:].rearrange("p i d -> p (i d)"))
+
+        def out_store_half(t, a):
+            h, s = UNITS[t]
+            nc.sync.dma_start(
+                out=out[0, h, HALF * s:HALF * (s + 1), :].rearrange("(r a i) d -> r a (i d)", a=2, i=2)[:, a, :],
+                in_=results[t][:, 2 * a:2 * a + 2, :].rearrange("p i d -> p (i d)"))
 
         tables_vector(0)
         w_tiles(0)
@@ -345,6 +353,8 @@ def tile_multiscaleretention_pa_kernel(tc, x, w, b, out):
             if live:
                 epi_even_bank(t)
             out_copy(t - 2, 0)
+            if t - 2 == units - 1:
+                out_store_half(t - 2, 0)
             prep(t, "s")
             prep(t, "v")
             prep(t, "g")
@@ -356,5 +366,8 @@ def tile_multiscaleretention_pa_kernel(tc, x, w, b, out):
             if live:
                 epi_odd_bank(t)
             out_copy(t - 2, 1)
-            out_store(t - 2)
+            if t - 2 == units - 1:
+                out_store_half(t - 2, 1)
+            else:
+                out_store(t - 2)
             prep(t, "s")

@@ -22,7 +22,7 @@ G = 4
 HALF = 512
 CHUNKS = ((0, 1), (1, 1), (2, 2), (4, 4))
 UNITS = ((0, 0), (1, 0), (0, 1), (1, 1)) + tuple((h, s) for h in range(2, H) for s in range(2))
-WI_ENGINE = "sssv"
+WI_ENGINE = "ssvs"
 RES_BUFS = 5
 LEAD = 4
 SPLIT = False
@@ -286,6 +286,8 @@ def tile_multiscaleretention_pa_kernel(tc, x, w, b, out):
             x_quant(0, g)
             w_quant1(0, g)
             mx_pass(0, g)
+            if g == 0:
+                tables_vector(1)
         bias_columns()
         w_tiles(1)
         x_transposes(1, 0)
@@ -304,7 +306,6 @@ def tile_multiscaleretention_pa_kernel(tc, x, w, b, out):
         mx_pass(1, 3)
         epi_even_bank(0)
         epi_odd_bank(0)
-        tables_vector(1)
         x_copies(1, 0)
         x_transposes(1, 2)
         x_copies(1, 1)
@@ -340,6 +341,8 @@ def tile_multiscaleretention_pa_kernel(tc, x, w, b, out):
                         w_quant2(h, a)
                         quantised.add((h, a))
 
+        prep(2, "s")
+        prep(2, "s")
         for t in range(2, units + 2):
             live = t < units
             if live:
@@ -349,7 +352,6 @@ def tile_multiscaleretention_pa_kernel(tc, x, w, b, out):
             out_transposes(t - 2, 0)
             if not SPLIT:
                 out_transposes(t - 2, 1)
-            quant_ready()
             if live:
                 epi_even_bank(t)
             out_copy(t - 2, 0)

@@ -24,7 +24,7 @@ CHUNKS = ((0, 1), (1, 1), (2, 2), (4, 4))
 UNITS = ((0, 0), (1, 0), (0, 1), (1, 1)) + tuple((h, s) for h in range(2, H) for s in range(2))
 WI_ENGINE = "ssvs"
 RES_BUFS = 5
-LEAD = 4
+LEAD = 3
 SPLIT = False
 
 
@@ -177,12 +177,10 @@ def tile_multiscaleretention_pa_kernel(tc, x, w, b, out):
         def tables_abs(s):
             c = slice(HALF * s, HALF * (s + 1))
             nc.scalar.activation(out=whole_f[:, c], in_=turns[:, c], func=ACT.Abs)
-            nc.gpsimd.tensor_scalar(out=whole_f[:, c], in0=whole_f[:, c], scalar1=-1.0, scalar2=0.25,
-                                    op0=ALU.mult, op1=ALU.add)
 
         def tables_cos(s):
             c = slice(HALF * s, HALF * (s + 1))
-            nc.scalar.activation(out=cos_t[:, c], in_=whole_f[:, c], func=ACT.Sin, scale=2.0 * math.pi)
+            nc.scalar.activation(out=cos_t[:, c], in_=whole_f[:, c], func=ACT.Sin, scale=-2.0 * math.pi, bias=0.5 * math.pi)
 
         def bias_columns():
             nc.vector.tensor_copy(out=b_f[:], in_=b_bf[:])
@@ -290,34 +288,34 @@ def tile_multiscaleretention_pa_kernel(tc, x, w, b, out):
                 tables_vector(1)
         bias_columns()
         w_tiles(1)
-        x_transposes(1, 0)
-        x_transposes(1, 1)
         w_interleave(1, 0, "s")
         w_interleave(1, 1, "v")
         w_quant1(1, 0)
         w_interleave(1, 2, "s")
         w_interleave(1, 3, "v")
         w_quant1(1, 1)
+        tables_sin(1)
+        tables_abs(1)
+        tables_cos(1)
         mx_pass(1, 0)
         mx_pass(1, 1)
         w_quant1(1, 2)
         w_quant1(1, 3)
         mx_pass(1, 2)
         mx_pass(1, 3)
+        x_transposes(1, 0)
+        x_transposes(1, 1)
         epi_even_bank(0)
         epi_odd_bank(0)
         x_copies(1, 0)
         x_transposes(1, 2)
         x_copies(1, 1)
         x_transposes(1, 3)
-        tables_sin(1)
         x_quant(1, 0)
         x_quant(1, 1)
         epi_even_bank(1)
         x_copies(1, 2)
-        tables_abs(1)
         x_copies(1, 3)
-        tables_cos(1)
         x_quant(1, 2)
         x_quant(1, 3)
         epi_odd_bank(1)

@@ -20,7 +20,7 @@ ACT = mybir.ActivationFunctionType
 P = 128
 G = 4
 HALF = 512
-CHUNKS = ((0, 1), (1, 1), (2, 2), (4, 4))
+CHUNKS = ((0, 2), (2, 2), (4, 4))
 UNITS = ((0, 0), (1, 0), (0, 1), (1, 1)) + tuple((h, s) for h in range(2, H) for s in range(2))
 WI_ENGINE = "ssvs"
 RES_BUFS = 5
@@ -78,10 +78,8 @@ def tile_multiscaleretention_pa_kernel(tc, x, w, b, out):
             load_x(0, g)
             load_w(0, g)
         for g in range(G):
-            load_w(1, g)
-        for g in range(G):
             load_x(1, g)
-        for c in range(2, len(CHUNKS)):
+        for c in range(1, len(CHUNKS)):
             for g in range(G):
                 load_w(c, g)
 
@@ -268,6 +266,7 @@ def tile_multiscaleretention_pa_kernel(tc, x, w, b, out):
 
         tables_vector(0)
         w_tiles(0)
+        w_tiles(1)
         x_transposes(0, 0)
         x_transposes(0, 1)
         for g in range(G):
@@ -281,28 +280,18 @@ def tile_multiscaleretention_pa_kernel(tc, x, w, b, out):
             if g + 2 < G:
                 x_transposes(0, g + 2)
             w_interleave(0, g, "v")
+            w_interleave(1, g, "s")
             x_quant(0, g)
             w_quant1(0, g)
             mx_pass(0, g)
+            w_quant1(1, g)
+            mx_pass(1, g)
             if g == 0:
                 tables_vector(1)
         bias_columns()
-        w_tiles(1)
-        w_interleave(1, 0, "s")
-        w_interleave(1, 1, "v")
-        w_quant1(1, 0)
-        w_interleave(1, 2, "s")
-        w_interleave(1, 3, "v")
-        w_quant1(1, 1)
         tables_sin(1)
         tables_abs(1)
         tables_cos(1)
-        mx_pass(1, 0)
-        mx_pass(1, 1)
-        w_quant1(1, 2)
-        w_quant1(1, 3)
-        mx_pass(1, 2)
-        mx_pass(1, 3)
         x_transposes(1, 0)
         x_transposes(1, 1)
         epi_even_bank(0)

@@ -127,8 +127,8 @@ def tile_multiscaleretention_pa_kernel(tc, x, w, b, out):
             if (h, g // 2) not in wg_tiles:
                 wg_tiles[(h, g // 2)] = wg_pool.tile([P, 2, 4 * D], BF16, name="wg", tag="wg", align_bytes=64)
             t = wg_tiles[(h, g // 2)]
-            dst = t[:, g % 2, :].rearrange("p (e j t) -> p e j t", e=2, t=4)
-            src = head_src[(h, g)].rearrange("p t (j e) -> p e j t", e=2)
+            dst = t[:, g % 2, :].rearrange("p (e j i t) -> p e j t i", e=2, i=4, t=4)
+            src = head_src[(h, g)].rearrange("p t (j i e) -> p e j t i", e=2, i=4)
             if eng == "s":
                 nc.scalar.copy(out=dst, in_=src)
             elif eng == "v":

@@ -22,10 +22,10 @@ G = 4
 HALF = 512
 CHUNKS = ((0, 2), (2, 2), (4, 4))
 UNITS = ((0, 0), (1, 0), (0, 1), (1, 1)) + tuple((h, s) for h in range(2, H) for s in range(2))
-WI_ENGINE = "ssvs"
 RES_BUFS = 5
-LEAD = 3
-SPLIT = False
+WI_ENGINE = ("ssss", "sgss", "sgss", "sgss", "sgss", "sgss")
+GP_ODD_FROM = 8
+LAST = 15
 
 
 def tile_multiscaleretention_pa_kernel(tc, x, w, b, out):
@@ -33,7 +33,7 @@ def tile_multiscaleretention_pa_kernel(tc, x, w, b, out):
     with ExitStack() as ctx:
         const = ctx.enter_context(tc.tile_pool(name="const", bufs=1))
         wg_pool = ctx.enter_context(tc.tile_pool(name="wg", bufs=4))
-        wc_pool = ctx.enter_context(tc.tile_pool(name="wc", bufs=3))
+        wc_pool = ctx.enter_context(tc.tile_pool(name="wc", bufs=5))
         ep3 = ctx.enter_context(tc.tile_pool(name="ep3", bufs=3))
         ep2 = ctx.enter_context(tc.tile_pool(name="ep2", bufs=2))
         res_pool = ctx.enter_context(tc.tile_pool(name="res", bufs=RES_BUFS))
@@ -49,18 +49,18 @@ def tile_multiscaleretention_pa_kernel(tc, x, w, b, out):
 
         ident = const.tile([P, P], F32, name="ident")
         make_identity(nc, ident[:])
-        n_iota = const.tile([P, N_TOK], F32, name="n_iota")
-        nc.gpsimd.iota(n_iota[:], pattern=[[HALF, 2], [1, 4], [4, P]], base=0,
+        n_iota = const.tile([P, HALF], F32, name="n_iota")
+        nc.gpsimd.iota(n_iota[:], pattern=[[1, 4], [4, P]], base=0,
                        channel_multiplier=0, allow_small_or_imprecise_dtypes=True)
 
-        xv = x[0].rearrange("(s r i) (g k) -> s g r i k", s=2, i=4, g=G)
+        xv = x[0].rearrange("(s r i) k -> s i r k", s=2, i=4)
         x_raw = {}
         head_src = {}
 
-        def load_x(s, g):
-            t = const.tile([P, 4, 512], BF16, name="x_raw%d%d" % (s, g))
-            nc.sync.dma_start(out=t[:], in_=xv[s, g])
-            x_raw[(s, g)] = t
+        def load_x(s, i):
+            t = const.tile([P, E], BF16, name="x_raw%d%d" % (s, i))
+            nc.sync.dma_start(out=t[:], in_=xv[s, i])
+            x_raw[(s, i)] = t
 
         def load_w(c, g):
             h0, nh = CHUNKS[c]
@@ -71,31 +71,33 @@ def tile_multiscaleretention_pa_kernel(tc, x, w, b, out):
             for hl in range(nh):
                 head_src[(h0 + hl, g)] = t[:, :, D * hl:D * (hl + 1)]
 
-        load_x(0, 0)
+        for i in range(4):
+            load_x(0, i)
         load_w(0, 0)
         nc.sync.dma_start(out=b_bf[:], in_=b.rearrange("(h j e) -> j h e", h=H, e=2))
         for g in range(1, G):
-            load_x(0, g)
             load_w(0, g)
-        for g in range(G):
-            load_x(1, g)
+        for i in range(4):
+            load_x(1, i)
         for c in range(1, len(CHUNKS)):
             for g in range(G):
                 load_w(c, g)
 
         ratio = 10000.0 ** (-1.0 / 127.0)
         frow = const.tile([P, P], F32, name="frow")
-        nc.vector.tensor_scalar(out=frow[:, 0:1], in0=ones[:], scalar1=1.0 / (2.0 * math.pi),
-                                scalar2=None, op0=ALU.mult)
-        m = 1
-        while m < P:
-            nc.vector.tensor_scalar(out=frow[:, m:2 * m], in0=frow[:, 0:m], scalar1=ratio ** m,
+        for m in range(4):
+            nc.vector.tensor_scalar(out=frow[:, m:m + 1], in0=ones[:], scalar1=ratio ** m / (2.0 * math.pi),
                                     scalar2=None, op0=ALU.mult)
-            m *= 2
+        for m in range(4, 16, 4):
+            nc.vector.tensor_scalar(out=frow[:, m:m + 4], in0=frow[:, 0:4], scalar1=ratio ** m,
+                                    scalar2=None, op0=ALU.mult)
+        for m in range(16, P, 16):
+            nc.vector.tensor_scalar(out=frow[:, m:m + 16], in0=frow[:, 0:16], scalar1=ratio ** m,
+                                    scalar2=None, op0=ALU.mult)
         fdiag = const.tile([P, P], F32, name="fdiag")
-        nc.vector.tensor_tensor(out=fdiag[:], in0=frow[:], in1=ident[:], op=ALU.mult)
         fcol = const.tile([P, 1], F32, name="fcol")
-        nc.vector.tensor_reduce(out=fcol[:], in_=fdiag[:], axis=mybir.AxisListType.X, op=ALU.add)
+        nc.vector.scalar_tensor_tensor(out=fdiag[:], in0=frow[:], scalar=1.0, in1=ident[:], op0=ALU.mult, op1=ALU.mult,
+                                       accum_out=fcol[:])
 
         xg = const.tile([P, G, 4 * HALF], BF16, name="xg", align_bytes=64)
         xg_w = xg[:].bitcast(F32).rearrange("p g (i r u) -> p g i r u", i=4, u=2)
@@ -103,22 +105,28 @@ def tile_multiscaleretention_pa_kernel(tc, x, w, b, out):
         xs = [const.tile([P, G, HALF], U8, name="xs%d" % s, align_bytes=64) for s in range(2)]
         xts = {}
 
-        def x_transposes(s, g):
+        def x_transposes(s, i):
+            words = x_raw[(s, i)][:].bitcast(F32)
             for a in range(2):
                 xt = tp_pool.tile([P, 2, 2, P], F32, name="xt", tag="tp")
-                for ii in range(2):
-                    words = x_raw[(s, g)][:, 2 * a + ii, :].bitcast(F32)
+                for gg in range(2):
+                    g = 2 * a + gg
                     for u in range(2):
-                        nc.tensor.transpose(xt[:, ii, u, :], words[:, u:256:2], ident[:])
-                xts[(s, g, a)] = xt
+                        nc.tensor.transpose(xt[:, gg, u, :], words[:, 256 * g + u:256 * (g + 1):2], ident[:])
+                xts[(s, i, a)] = xt
 
-        def x_copies(s, g):
-            for a in range(2):
-                nc.scalar.copy(out=xg_w[:, g, 2 * a:2 * a + 2, :, :],
-                               in_=xts[(s, g, a)][:].rearrange("p i u r -> p i r u"))
+        def x_copy(s, i, a, eng):
+            dst = xg_w[:, 2 * a:2 * a + 2, i, :, :]
+            src = xts[(s, i, a)][:].rearrange("p g u r -> p g r u")
+            if eng == "s":
+                nc.scalar.copy(out=dst, in_=src)
+            else:
+                nc.vector.tensor_copy(out=dst, in_=src)
 
-        def x_quant(s, g):
-            nc.vector.quantize_mx(out=xc[s][:, g, :].bitcast(E5X4), scales=xs[s][:, g, :], in_=xg[:, g, :])
+        def x_quant(s, i):
+            for g in range(G):
+                nc.vector.quantize_mx(out=xc[s][:, g, P * i:P * (i + 1)].bitcast(E5X4),
+                                      scales=xs[s][:, g, P * i:P * (i + 1)], in_=xg[:, g, 512 * i:512 * (i + 1)])
 
         w_codes = {}
         wg_tiles = {}
@@ -158,15 +166,24 @@ def tile_multiscaleretention_pa_kernel(tc, x, w, b, out):
         cos_t = const.tile([P, N_TOK], F32, name="cos_t")
         sin_t = const.tile([P, N_TOK], F32, name="sin_t")
         turns = const.tile([P, N_TOK], F32, name="turns")
-        whole_i = const.tile([P, N_TOK], I32, name="whole_i")
-        whole_f = const.tile([P, N_TOK], F32, name="whole_f")
         b_f = const.tile([P, H, 2], F32, name="b_f")
 
-        def tables_vector(s):
-            c = slice(HALF * s, HALF * (s + 1))
-            nc.vector.tensor_scalar(out=whole_i[:, c], in0=n_iota[:, c], scalar1=fcol[:, 0:1], scalar2=None, op0=ALU.mult)
-            nc.vector.scalar_tensor_tensor(out=turns[:, c], in0=n_iota[:, c], scalar=fcol[:, 0:1], in1=whole_i[:, c],
+        whole_i = const.tile([P, HALF], I32, name="whole_i")
+        step_i = const.tile([P, 1], I32, name="step_i")
+        step_t = const.tile([P, 1], F32, name="step_t")
+
+        def tables_vector0():
+            nc.vector.tensor_scalar(out=whole_i[:], in0=n_iota[:], scalar1=fcol[:, 0:1], scalar2=None, op0=ALU.mult)
+            nc.vector.tensor_scalar(out=step_i[:], in0=fcol[:], scalar1=float(HALF), scalar2=None, op0=ALU.mult)
+            nc.vector.scalar_tensor_tensor(out=turns[:, 0:HALF], in0=n_iota[:], scalar=fcol[:, 0:1], in1=whole_i[:],
                                            op0=ALU.mult, op1=ALU.subtract)
+            nc.vector.scalar_tensor_tensor(out=step_t[:], in0=fcol[:], scalar=float(HALF), in1=step_i[:],
+                                           op0=ALU.mult, op1=ALU.subtract)
+
+        def tables_vector1():
+            nc.vector.tensor_scalar(out=whole_i[:], in0=turns[:, 0:HALF], scalar1=step_t[:, 0:1], scalar2=None, op0=ALU.add)
+            nc.vector.scalar_tensor_tensor(out=turns[:, HALF:N_TOK], in0=turns[:, 0:HALF], scalar=step_t[:, 0:1], in1=whole_i[:],
+                                           op0=ALU.add, op1=ALU.subtract)
 
         def tables_sin(s):
             c = slice(HALF * s, HALF * (s + 1))
@@ -174,11 +191,11 @@ def tile_multiscaleretention_pa_kernel(tc, x, w, b, out):
 
         def tables_abs(s):
             c = slice(HALF * s, HALF * (s + 1))
-            nc.scalar.activation(out=whole_f[:, c], in_=turns[:, c], func=ACT.Abs)
+            nc.scalar.activation(out=cos_t[:, c], in_=turns[:, c], func=ACT.Abs)
 
         def tables_cos(s):
             c = slice(HALF * s, HALF * (s + 1))
-            nc.scalar.activation(out=cos_t[:, c], in_=whole_f[:, c], func=ACT.Sin, scale=-2.0 * math.pi, bias=0.5 * math.pi)
+            nc.scalar.activation(out=cos_t[:, c], in_=cos_t[:, c], func=ACT.Sin, scale=-2.0 * math.pi, bias=0.5 * math.pi)
 
         def bias_columns():
             nc.vector.tensor_copy(out=b_f[:], in_=b_bf[:])
@@ -208,49 +225,56 @@ def tile_multiscaleretention_pa_kernel(tc, x, w, b, out):
             for g in range(G):
                 mx_one(t, e, g)
 
-        def epi_even_bank(t):
+        def product(t, e, table, tag, c0, c1):
             h, s = UNITS[t]
-            ec = ep3.tile([P, HALF], F32, name="ec", tag="ec")
-            es = ep3.tile([P, HALF], F32, name="es", tag="es")
-            be = b_f[:, h, 0:1]
-            nc.vector.scalar_tensor_tensor(out=ec[:], in0=accs[(t, 0)][:], scalar=be,
-                                           in1=cos_t[:, HALF * s:HALF * (s + 1)], op0=ALU.add, op1=ALU.mult)
-            nc.vector.scalar_tensor_tensor(out=es[:], in0=accs[(t, 0)][:], scalar=be,
-                                           in1=sin_t[:, HALF * s:HALF * (s + 1)], op0=ALU.add, op1=ALU.mult)
-            rot[t] = [ec, es]
+            if (t, tag) not in rot:
+                pool = ep2 if tag == "os_" else ep3
+                rot[(t, tag)] = pool.tile([P, HALF], F32, name=tag, tag=tag)
+            nc.vector.scalar_tensor_tensor(out=rot[(t, tag)][:, c0:c1], in0=accs[(t, e)][:, c0:c1], scalar=b_f[:, h, e:e + 1],
+                                           in1=table[:, HALF * s + c0:HALF * s + c1], op0=ALU.add, op1=ALU.mult)
 
-        def epi_odd_bank(t):
-            h, s = UNITS[t]
-            os_ = ep2.tile([P, HALF], F32, name="os_", tag="os_")
-            oc = ep3.tile([P, HALF], F32, name="oc", tag="oc")
-            bo = b_f[:, h, 1:2]
-            nc.vector.scalar_tensor_tensor(out=os_[:], in0=accs[(t, 1)][:], scalar=bo,
-                                           in1=sin_t[:, HALF * s:HALF * (s + 1)], op0=ALU.add, op1=ALU.mult)
-            nc.vector.scalar_tensor_tensor(out=oc[:], in0=accs[(t, 1)][:], scalar=bo,
-                                           in1=cos_t[:, HALF * s:HALF * (s + 1)], op0=ALU.add, op1=ALU.mult)
-            ec = rot[t][0]
-            (nc.vector if t == len(UNITS) - 1 else nc.gpsimd).tensor_tensor(out=ec[:], in0=ec[:], in1=os_[:], op=ALU.subtract)
-            rot[t].append(oc)
+        def products_sub(t, c0=0, c1=HALF):
+            product(t, 1, sin_t, "os_", c0, c1)
+            product(t, 0, cos_t, "ec", c0, c1)
+
+        def products_add(t, c0=0, c1=HALF):
+            product(t, 0, sin_t, "es", c0, c1)
+            product(t, 1, cos_t, "oc", c0, c1)
+
+        def subtract(t, eng, c0=0, c1=HALF):
+            ec = rot[(t, "ec")]
+            eng.tensor_tensor(out=ec[:, c0:c1], in0=ec[:, c0:c1], in1=rot[(t, "os_")][:, c0:c1], op=ALU.subtract)
+
+        def add(t, eng, c0=0, c1=HALF):
+            oc = rot[(t, "oc")]
+            eng.tensor_tensor(out=oc[:, c0:c1], in0=oc[:, c0:c1], in1=rot[(t, "es")][:, c0:c1], op=ALU.add)
 
         def out_transposes(t, a):
-            ec, es, oc = rot[t]
+            ec, es, oc = (rot[(t, tag)] for tag in ("ec", "es", "oc"))
             ot = tp_pool.tile([P, 2, 2, P], F32, name="ot", tag="tp")
             for ii in range(2):
                 i = 2 * a + ii
                 nc.tensor.transpose(ot[:, ii, 0, :], ec[:, P * i:P * (i + 1)], ident[:])
-                nc.tensor.matmul(ot[:, ii, 1, :], lhsT=oc[:, P * i:P * (i + 1)], rhs=ident[:],
-                                 is_transpose=True, start=True, stop=False)
-                nc.tensor.matmul(ot[:, ii, 1, :], lhsT=es[:, P * i:P * (i + 1)], rhs=ident[:],
-                                 is_transpose=True, start=False, stop=True)
+                if GP_ODD_FROM <= t < LAST:
+                    nc.tensor.transpose(ot[:, ii, 1, :], oc[:, P * i:P * (i + 1)], ident[:])
+                else:
+                    nc.tensor.matmul(ot[:, ii, 1, :], lhsT=oc[:, P * i:P * (i + 1)], rhs=ident[:],
+                                     is_transpose=True, start=True, stop=False)
+                    nc.tensor.matmul(ot[:, ii, 1, :], lhsT=es[:, P * i:P * (i + 1)], rhs=ident[:],
+                                     is_transpose=True, start=False, stop=True)
             ots[(t, a)] = ot
 
         results = {}
 
-        def out_copy(t, a):
+        def out_copy(t, a, eng="s"):
             if a == 0:
                 results[t] = res_pool.tile([P, 4, D], F32, name="res", tag="res")
-            nc.scalar.copy(out=results[t][:, 2 * a:2 * a + 2, :].rearrange("p i (j e) -> p i j e", e=2),
-                           in_=ots[(t, a)][:].rearrange("p i e j -> p i j e"))
+            dst = results[t][:, 2 * a:2 * a + 2, :].rearrange("p i (j e) -> p i j e", e=2)
+            src = ots[(t, a)][:].rearrange("p i e j -> p i j e")
+            if eng == "s":
+                nc.scalar.copy(out=dst, in_=src)
+            else:
+                nc.vector.tensor_copy(out=dst, in_=src)
 
         def out_store(t):
             h, s = UNITS[t]
@@ -264,60 +288,71 @@ def tile_multiscaleretention_pa_kernel(tc, x, w, b, out):
                 out=out[0, h, HALF * s:HALF * (s + 1), :].rearrange("(r a i) d -> r a (i d)", a=2, i=2)[:, a, :],
                 in_=results[t][:, 2 * a:2 * a + 2, :].rearrange("p i d -> p (i d)"))
 
-        tables_vector(0)
+        tables_vector0()
+        tables_sin(0)
+        tables_vector1()
         w_tiles(0)
         w_tiles(1)
         x_transposes(0, 0)
         x_transposes(0, 1)
-        for g in range(G):
-            x_copies(0, g)
-            if g == 0:
-                tables_sin(0)
-            if g == 1:
+        for i in range(4):
+            x_copy(0, i, 0, "s")
+            x_copy(0, i, 1, "v" if i in (1, 2) else "s")
+            if i + 2 < 4:
+                x_transposes(0, i + 2)
+            if i == 1:
                 tables_abs(0)
-            if g == 2:
+            if i == 2:
                 tables_cos(0)
-            if g + 2 < G:
-                x_transposes(0, g + 2)
+            x_quant(0, i)
+        for g in range(G):
             w_interleave(0, g, "v")
             w_interleave(1, g, "s")
-            x_quant(0, g)
+            if g > 0:
+                w_quant1(1, g - 1)
+                mx_pass(1, g - 1)
             w_quant1(0, g)
             mx_pass(0, g)
-            w_quant1(1, g)
-            mx_pass(1, g)
-            if g == 0:
-                tables_vector(1)
-        bias_columns()
         tables_sin(1)
         tables_abs(1)
-        tables_cos(1)
         x_transposes(1, 0)
+        w_quant1(1, G - 1)
+        mx_pass(1, G - 1)
+        bias_columns()
         x_transposes(1, 1)
-        epi_even_bank(0)
-        epi_odd_bank(0)
-        x_copies(1, 0)
+        x_copy(1, 0, 0, "s")
+        x_copy(1, 0, 1, "s")
         x_transposes(1, 2)
-        x_copies(1, 1)
-        x_transposes(1, 3)
+        products_sub(0)
+        x_copy(1, 1, 0, "s")
+        x_copy(1, 1, 1, "s")
+        subtract(0, nc.gpsimd)
+        products_add(0)
         x_quant(1, 0)
+        tables_cos(1)
+        x_transposes(1, 3)
         x_quant(1, 1)
-        epi_even_bank(1)
-        x_copies(1, 2)
-        x_copies(1, 3)
+        x_copy(1, 2, 0, "s")
+        x_copy(1, 2, 1, "s")
         x_quant(1, 2)
+        x_copy(1, 3, 0, "s")
+        x_copy(1, 3, 1, "s")
         x_quant(1, 3)
-        epi_odd_bank(1)
+        out_transposes(0, 0)
+        out_transposes(0, 1)
+        products_sub(1)
+        subtract(1, nc.gpsimd)
+        products_add(1)
         units = len(UNITS)
-        queue = dict((k, [(h, g) for h in range(2, H) for g in range(G) if WI_ENGINE[g] == k]) for k in "svg")
-        done = set()
+        queue = dict((k, [(h, g) for h in range(2, H) for g in range(G) if WI_ENGINE[h - 2][g] == k]) for k in "svg")
+        done = []
         quantised = set()
 
-        def prep(t, k):
-            if queue[k] and queue[k][0][0] <= (t + LEAD) // 2:
+        def prep(k):
+            if queue[k]:
                 h, g = queue[k].pop(0)
                 w_interleave(h, g, k)
-                done.add((h, g))
+                done.append((h, g))
 
         def quant_ready():
             for h in range(2, H):
@@ -327,36 +362,43 @@ def tile_multiscaleretention_pa_kernel(tc, x, w, b, out):
                             w_tiles(h)
                         w_quant2(h, a)
                         quantised.add((h, a))
+                        return
 
-        prep(2, "s")
-        prep(2, "s")
+        for g in range(G):
+            prep("s")
+        quant_ready()
         for t in range(2, units + 2):
-            live = t < units
-            if live:
-                mx_bank(t, 0)
-                if not SPLIT:
-                    mx_bank(t, 1)
-            out_transposes(t - 2, 0)
-            if not SPLIT:
+            if t < units:
+                for e in (1, 0) if t < LAST else (0, 1):
+                    mx_bank(t, e)
+            if t > 2:
+                out_transposes(t - 2, 0)
                 out_transposes(t - 2, 1)
-            if live:
-                epi_even_bank(t)
+            if t < LAST:
+                products_sub(t)
+                if t > 2:
+                    quant_ready()
+                subtract(t, nc.gpsimd)
+                prep("g")
+                products_add(t)
+                if t == 2:
+                    quant_ready()
+                if t >= GP_ODD_FROM:
+                    add(t, nc.gpsimd)
+            elif t == LAST:
+                product(t, 0, cos_t, "ec", 0, HALF)
+                product(t, 0, sin_t, "es", 0, HALF)
+                for c in (0, 256):
+                    product(t, 1, sin_t, "os_", c, c + 256)
+                    product(t, 1, cos_t, "oc", c, c + 256)
+                    subtract(t, nc.vector, c, c + 256)
             out_copy(t - 2, 0)
-            if t - 2 == units - 1:
+            if t - 2 == LAST:
                 out_store_half(t - 2, 0)
-            prep(t, "s")
-            prep(t, "v")
-            prep(t, "g")
-            if live and SPLIT:
-                mx_bank(t, 1)
-            if SPLIT:
-                out_transposes(t - 2, 1)
-            quant_ready()
-            if live:
-                epi_odd_bank(t)
+            prep("s")
             out_copy(t - 2, 1)
-            if t - 2 == units - 1:
+            if t - 2 == LAST:
                 out_store_half(t - 2, 1)
             else:
                 out_store(t - 2)
-            prep(t, "s")
+            prep("s")

@@ -23,8 +23,9 @@ HALF = 512
 CHUNKS = ((0, 2), (2, 2), (4, 4))
 UNITS = ((0, 0), (1, 0), (0, 1), (1, 1)) + tuple((h, s) for h in range(2, H) for s in range(2))
 RES_BUFS = 5
-WI_ENGINE = ("ssss", "sgss", "sgss", "sgss", "sgss", "sgss")
-GP_ODD_FROM = 8
+LEAD = 5
+WI_ENGINE = ("ssss", "svss", "svss", "svss", "svss", "svss")
+GP_ODD_FROM = 4
 LAST = 15
 
 
@@ -348,8 +349,8 @@ def tile_multiscaleretention_pa_kernel(tc, x, w, b, out):
         done = []
         quantised = set()
 
-        def prep(k):
-            if queue[k]:
+        def prep(k, t=2):
+            if queue[k] and queue[k][0][0] <= (t + LEAD) // 2:
                 h, g = queue[k].pop(0)
                 w_interleave(h, g, k)
                 done.append((h, g))
@@ -378,8 +379,9 @@ def tile_multiscaleretention_pa_kernel(tc, x, w, b, out):
                 products_sub(t)
                 if t > 2:
                     quant_ready()
+                prep("v", t)
                 subtract(t, nc.gpsimd)
-                prep("g")
+                prep("g", t)
                 products_add(t)
                 if t == 2:
                     quant_ready()
@@ -395,10 +397,10 @@ def tile_multiscaleretention_pa_kernel(tc, x, w, b, out):
             out_copy(t - 2, 0)
             if t - 2 == LAST:
                 out_store_half(t - 2, 0)
-            prep("s")
+            prep("s", t)
             out_copy(t - 2, 1)
             if t - 2 == LAST:
                 out_store_half(t - 2, 1)
             else:
                 out_store(t - 2)
-            prep("s")
+            prep("s", t)

@@ -24,8 +24,8 @@ CHUNKS = ((0, 2), (2, 2), (4, 4))
 UNITS = ((0, 0), (1, 0), (0, 1), (1, 1)) + tuple((h, s) for h in range(2, H) for s in range(2))
 RES_BUFS = 5
 LEAD = 5
-WI_ENGINE = ("ssss", "svss", "svss", "svss", "svss", "svss")
-GP_ODD_FROM = 4
+WI_ENGINE = ("ssss", "svsv", "svss", "ssss", "ssss", "ssss")
+GP_ODD_FROM = 6
 LAST = 15
 
 
@@ -74,12 +74,14 @@ def tile_multiscaleretention_pa_kernel(tc, x, w, b, out):
 
         for i in range(4):
             load_x(0, i)
+        load_x(1, 0)
+        load_x(1, 1)
         load_w(0, 0)
         nc.sync.dma_start(out=b_bf[:], in_=b.rearrange("(h j e) -> j h e", h=H, e=2))
         for g in range(1, G):
             load_w(0, g)
-        for i in range(4):
-            load_x(1, i)
+        load_x(1, 2)
+        load_x(1, 3)
         for c in range(1, len(CHUNKS)):
             for g in range(G):
                 load_w(c, g)
@@ -306,38 +308,41 @@ def tile_multiscaleretention_pa_kernel(tc, x, w, b, out):
             if i == 2:
                 tables_cos(0)
             x_quant(0, i)
+        x_transposes(1, 0)
+        w_interleave(0, 0, "v")
+        w_interleave(1, 0, "s")
+        x_transposes(1, 1)
+        x_copy(1, 0, 0, "s")
+        x_copy(1, 0, 1, "s")
         for g in range(G):
-            w_interleave(0, g, "v")
-            w_interleave(1, g, "s")
             if g > 0:
+                w_interleave(0, g, "v")
+                w_interleave(1, g, "s")
                 w_quant1(1, g - 1)
                 mx_pass(1, g - 1)
             w_quant1(0, g)
             mx_pass(0, g)
-        tables_sin(1)
-        tables_abs(1)
-        x_transposes(1, 0)
+            if g == 1:
+                x_copy(1, 1, 0, "s")
+                x_copy(1, 1, 1, "s")
+                x_quant(1, 0)
+        x_transposes(1, 2)
         w_quant1(1, G - 1)
         mx_pass(1, G - 1)
-        bias_columns()
-        x_transposes(1, 1)
-        x_copy(1, 0, 0, "s")
-        x_copy(1, 0, 1, "s")
-        x_transposes(1, 2)
-        products_sub(0)
-        x_copy(1, 1, 0, "s")
-        x_copy(1, 1, 1, "s")
-        subtract(0, nc.gpsimd)
-        products_add(0)
-        x_quant(1, 0)
-        tables_cos(1)
         x_transposes(1, 3)
-        x_quant(1, 1)
+        tables_sin(1)
+        tables_abs(1)
+        bias_columns()
+        products_sub(0)
         x_copy(1, 2, 0, "s")
         x_copy(1, 2, 1, "s")
-        x_quant(1, 2)
+        subtract(0, nc.gpsimd)
+        products_add(0)
+        tables_cos(1)
         x_copy(1, 3, 0, "s")
         x_copy(1, 3, 1, "s")
+        x_quant(1, 1)
+        x_quant(1, 2)
         x_quant(1, 3)
         out_transposes(0, 0)
         out_transposes(0, 1)
@@ -372,9 +377,12 @@ def tile_multiscaleretention_pa_kernel(tc, x, w, b, out):
             if t < units:
                 for e in (1, 0) if t < LAST else (0, 1):
                     mx_bank(t, e)
-            if t > 2:
+            if 2 < t != LAST:
                 out_transposes(t - 2, 0)
                 out_transposes(t - 2, 1)
+            if t == LAST - 1:
+                out_transposes(t - 1, 0)
+                out_transposes(t - 1, 1)
             if t < LAST:
                 products_sub(t)
                 if t > 2:
@@ -398,7 +406,7 @@ def tile_multiscaleretention_pa_kernel(tc, x, w, b, out):
             if t - 2 == LAST:
                 out_store_half(t - 2, 0)
             prep("s", t)
-            out_copy(t - 2, 1)
+            out_copy(t - 2, 1, "v" if t - 2 == LAST else "s")
             if t - 2 == LAST:
                 out_store_half(t - 2, 1)
             else:

@@ -25,8 +25,9 @@ UNITS = ((0, 0), (1, 0), (0, 1), (1, 1)) + tuple((h, s) for h in range(2, H) for
 RES_BUFS = 5
 LEAD = 5
 WI_ENGINE = ("ssss", "svsv", "svss", "ssss", "ssss", "ssss")
-GP_ODD_FROM = 6
+GP_ODD_FROM = 4
 LAST = 15
+PAIR_FROM = 8
 
 
 def tile_multiscaleretention_pa_kernel(tc, x, w, b, out):
@@ -36,7 +37,6 @@ def tile_multiscaleretention_pa_kernel(tc, x, w, b, out):
         wg_pool = ctx.enter_context(tc.tile_pool(name="wg", bufs=4))
         wc_pool = ctx.enter_context(tc.tile_pool(name="wc", bufs=5))
         ep3 = ctx.enter_context(tc.tile_pool(name="ep3", bufs=3))
-        ep2 = ctx.enter_context(tc.tile_pool(name="ep2", bufs=2))
         res_pool = ctx.enter_context(tc.tile_pool(name="res", bufs=RES_BUFS))
         acc_pool = ctx.enter_context(tc.psum_pool(name="acc", bufs=4))
         tp_pool = ctx.enter_context(tc.psum_pool(name="tp", bufs=4))
@@ -127,9 +127,10 @@ def tile_multiscaleretention_pa_kernel(tc, x, w, b, out):
                 nc.vector.tensor_copy(out=dst, in_=src)
 
         def x_quant(s, i):
+            c = slice(P * i, P * (i + 2))
             for g in range(G):
-                nc.vector.quantize_mx(out=xc[s][:, g, P * i:P * (i + 1)].bitcast(E5X4),
-                                      scales=xs[s][:, g, P * i:P * (i + 1)], in_=xg[:, g, 512 * i:512 * (i + 1)])
+                nc.vector.quantize_mx(out=xc[s][:, g, c].bitcast(E5X4), scales=xs[s][:, g, c],
+                                      in_=xg[:, g, 512 * i:512 * (i + 2)])
 
         w_codes = {}
         wg_tiles = {}
@@ -166,8 +167,7 @@ def tile_multiscaleretention_pa_kernel(tc, x, w, b, out):
                 scales=sca[:, 2 * a:2 * a + 2, :].rearrange("p g c -> p (g c)"),
                 in_=wg_tiles[(h, a)][:].rearrange("p g c -> p (g c)"))
 
-        cos_t = const.tile([P, N_TOK], F32, name="cos_t")
-        sin_t = const.tile([P, N_TOK], F32, name="sin_t")
+        table = const.tile([P, 2, 2, HALF], F32, name="table")
         turns = const.tile([P, N_TOK], F32, name="turns")
         b_f = const.tile([P, H, 2], F32, name="b_f")
 
@@ -190,15 +190,15 @@ def tile_multiscaleretention_pa_kernel(tc, x, w, b, out):
 
         def tables_sin(s):
             c = slice(HALF * s, HALF * (s + 1))
-            nc.scalar.activation(out=sin_t[:, c], in_=turns[:, c], func=ACT.Sin, scale=2.0 * math.pi)
+            nc.scalar.activation(out=table[:, s, 1, :], in_=turns[:, c], func=ACT.Sin, scale=2.0 * math.pi)
 
         def tables_abs(s):
             c = slice(HALF * s, HALF * (s + 1))
-            nc.scalar.activation(out=cos_t[:, c], in_=turns[:, c], func=ACT.Abs)
+            nc.scalar.activation(out=table[:, s, 0, :], in_=turns[:, c], func=ACT.Abs)
 
         def tables_cos(s):
             c = slice(HALF * s, HALF * (s + 1))
-            nc.scalar.activation(out=cos_t[:, c], in_=cos_t[:, c], func=ACT.Sin, scale=-2.0 * math.pi, bias=0.5 * math.pi)
+            nc.scalar.activation(out=table[:, s, 0, :], in_=table[:, s, 0, :], func=ACT.Sin, scale=-2.0 * math.pi, bias=0.5 * math.pi)
 
         def bias_columns():
             nc.vector.tensor_copy(out=b_f[:], in_=b_bf[:])
@@ -228,32 +228,32 @@ def tile_multiscaleretention_pa_kernel(tc, x, w, b, out):
             for g in range(G):
                 mx_one(t, e, g)
 
-        def product(t, e, table, tag, c0, c1):
+        def rotated(t, e):
+            if (t, e) not in rot:
+                rot[(t, e)] = ep3.tile([P, 2, HALF], F32, name="rot%d" % e, tag="rot%d" % e)
+            return rot[(t, e)]
+
+        def product(t, e, k):
             h, s = UNITS[t]
-            if (t, tag) not in rot:
-                pool = ep2 if tag == "os_" else ep3
-                rot[(t, tag)] = pool.tile([P, HALF], F32, name=tag, tag=tag)
-            nc.vector.scalar_tensor_tensor(out=rot[(t, tag)][:, c0:c1], in0=accs[(t, e)][:, c0:c1], scalar=b_f[:, h, e:e + 1],
-                                           in1=table[:, HALF * s + c0:HALF * s + c1], op0=ALU.add, op1=ALU.mult)
+            nc.vector.scalar_tensor_tensor(out=rotated(t, e)[:, k, :], in0=accs[(t, e)][:], scalar=b_f[:, h, e:e + 1],
+                                           in1=table[:, s, k, :], op0=ALU.add, op1=ALU.mult)
 
-        def products_sub(t, c0=0, c1=HALF):
-            product(t, 1, sin_t, "os_", c0, c1)
-            product(t, 0, cos_t, "ec", c0, c1)
-
-        def products_add(t, c0=0, c1=HALF):
-            product(t, 0, sin_t, "es", c0, c1)
-            product(t, 1, cos_t, "oc", c0, c1)
+        def products(t, e, c0=0, c1=HALF):
+            h, s = UNITS[t]
+            nc.vector.scalar_tensor_tensor(out=rotated(t, e)[:, :, c0:c1],
+                                           in0=accs[(t, e)][:, c0:c1].unsqueeze(1).to_broadcast([P, 2, c1 - c0]),
+                                           scalar=b_f[:, h, e:e + 1], in1=table[:, s, :, c0:c1], op0=ALU.add, op1=ALU.mult)
 
         def subtract(t, eng, c0=0, c1=HALF):
-            ec = rot[(t, "ec")]
-            eng.tensor_tensor(out=ec[:, c0:c1], in0=ec[:, c0:c1], in1=rot[(t, "os_")][:, c0:c1], op=ALU.subtract)
+            ec, os_ = rot[(t, 0)][:, 0, c0:c1], rot[(t, 1)][:, 1, c0:c1]
+            eng.tensor_tensor(out=ec, in0=ec, in1=os_, op=ALU.subtract)
 
         def add(t, eng, c0=0, c1=HALF):
-            oc = rot[(t, "oc")]
-            eng.tensor_tensor(out=oc[:, c0:c1], in0=oc[:, c0:c1], in1=rot[(t, "es")][:, c0:c1], op=ALU.add)
+            oc, es = rot[(t, 1)][:, 0, c0:c1], rot[(t, 0)][:, 1, c0:c1]
+            eng.tensor_tensor(out=oc, in0=oc, in1=es, op=ALU.add)
 
         def out_transposes(t, a):
-            ec, es, oc = (rot[(t, tag)] for tag in ("ec", "es", "oc"))
+            ec, es, oc = rot[(t, 0)][:, 0, :], rot[(t, 0)][:, 1, :], rot[(t, 1)][:, 0, :]
             ot = tp_pool.tile([P, 2, 2, P], F32, name="ot", tag="tp")
             for ii in range(2):
                 i = 2 * a + ii
@@ -307,9 +307,11 @@ def tile_multiscaleretention_pa_kernel(tc, x, w, b, out):
                 tables_abs(0)
             if i == 2:
                 tables_cos(0)
-            x_quant(0, i)
+            if i == 3:
+                w_interleave(0, 0, "v")
+            if i % 2 == 1:
+                x_quant(0, i - 1)
         x_transposes(1, 0)
-        w_interleave(0, 0, "v")
         w_interleave(1, 0, "s")
         x_transposes(1, 1)
         x_copy(1, 0, 0, "s")
@@ -325,6 +327,7 @@ def tile_multiscaleretention_pa_kernel(tc, x, w, b, out):
             if g == 1:
                 x_copy(1, 1, 0, "s")
                 x_copy(1, 1, 1, "s")
+            if g == 2:
                 x_quant(1, 0)
         x_transposes(1, 2)
         w_quant1(1, G - 1)
@@ -333,22 +336,24 @@ def tile_multiscaleretention_pa_kernel(tc, x, w, b, out):
         tables_sin(1)
         tables_abs(1)
         bias_columns()
-        products_sub(0)
+        product(0, 0, 0)
+        product(0, 1, 1)
         x_copy(1, 2, 0, "s")
         x_copy(1, 2, 1, "s")
         subtract(0, nc.gpsimd)
-        products_add(0)
+        product(0, 0, 1)
+        product(0, 1, 0)
         tables_cos(1)
         x_copy(1, 3, 0, "s")
         x_copy(1, 3, 1, "s")
-        x_quant(1, 1)
         x_quant(1, 2)
-        x_quant(1, 3)
         out_transposes(0, 0)
         out_transposes(0, 1)
-        products_sub(1)
+        product(1, 0, 0)
+        product(1, 1, 1)
         subtract(1, nc.gpsimd)
-        products_add(1)
+        product(1, 0, 1)
+        product(1, 1, 0)
         units = len(UNITS)
         queue = dict((k, [(h, g) for h in range(2, H) for g in range(G) if WI_ENGINE[h - 2][g] == k]) for k in "svg")
         done = []
@@ -374,33 +379,34 @@ def tile_multiscaleretention_pa_kernel(tc, x, w, b, out):
             prep("s")
         quant_ready()
         for t in range(2, units + 2):
-            if t < units:
-                for e in (1, 0) if t < LAST else (0, 1):
-                    mx_bank(t, e)
-            if 2 < t != LAST:
-                out_transposes(t - 2, 0)
-                out_transposes(t - 2, 1)
-            if t == LAST - 1:
-                out_transposes(t - 1, 0)
-                out_transposes(t - 1, 1)
+            if t < PAIR_FROM:
+                multiply, transpose = (t,), (t - 2,)
+            elif t < LAST - 1:
+                multiply, transpose = ((t, t + 1), (t - 2, t - 1)) if t % 2 == 0 else ((), ())
+            elif t <= LAST:
+                multiply, transpose = (t,), (t - 2,)
+            else:
+                multiply, transpose = (), (t - 2,)
+            for u in multiply:
+                mx_bank(u, 0)
+                mx_bank(u, 1)
+            for u in transpose:
+                if u > 0:
+                    out_transposes(u, 0)
+                    out_transposes(u, 1)
             if t < LAST:
-                products_sub(t)
-                if t > 2:
-                    quant_ready()
+                products(t, 0)
+                product(t, 1, 1)
+                quant_ready()
                 prep("v", t)
                 subtract(t, nc.gpsimd)
-                prep("g", t)
-                products_add(t)
-                if t == 2:
-                    quant_ready()
+                product(t, 1, 0)
                 if t >= GP_ODD_FROM:
                     add(t, nc.gpsimd)
             elif t == LAST:
-                product(t, 0, cos_t, "ec", 0, HALF)
-                product(t, 0, sin_t, "es", 0, HALF)
+                products(t, 0)
                 for c in (0, 256):
-                    product(t, 1, sin_t, "os_", c, c + 256)
-                    product(t, 1, cos_t, "oc", c, c + 256)
+                    products(t, 1, c, c + 256)
                     subtract(t, nc.vector, c, c + 256)
             out_copy(t - 2, 0)
             if t - 2 == LAST:

from contextlib import ExitStack
import math

import concourse.mybir as mybir
from concourse.masks import make_identity

N_TOK, E, H, D = 1024, 2048, 8, 256
FLOPS = 2 * N_TOK * E * E

F32 = mybir.dt.float32
BF16 = mybir.dt.bfloat16
I32 = mybir.dt.int32
U32 = mybir.dt.uint32
U8 = mybir.dt.uint8
E4X4 = mybir.dt.float8_e4m3fn_x4
E5X4 = mybir.dt.float8_e5m2_x4
ALU = mybir.AluOpType
ACT = mybir.ActivationFunctionType

P = 128
G = 4
HALF = 512
CHUNKS = ((0, 2), (2, 2), (4, 4))
UNITS = ((0, 0), (1, 0), (0, 1), (1, 1)) + tuple((h, s) for h in range(2, H) for s in range(2))
RES_BUFS = 5
LEAD = 5
WI_ENGINE = ("ssss", "svsv", "svss", "ssss", "ssss", "ssss")
GP_ODD_FROM = 4
LAST = 15
PAIR_FROM = 8


def tile_multiscaleretention_pa_kernel(tc, x, w, b, out):
    nc = tc.nc
    with ExitStack() as ctx:
        const = ctx.enter_context(tc.tile_pool(name="const", bufs=1))
        wg_pool = ctx.enter_context(tc.tile_pool(name="wg", bufs=4))
        wc_pool = ctx.enter_context(tc.tile_pool(name="wc", bufs=5))
        ep3 = ctx.enter_context(tc.tile_pool(name="ep3", bufs=3))
        res_pool = ctx.enter_context(tc.tile_pool(name="res", bufs=RES_BUFS))
        acc_pool = ctx.enter_context(tc.psum_pool(name="acc", bufs=4))
        tp_pool = ctx.enter_context(tc.psum_pool(name="tp", bufs=4))
        ctx.enter_context(tc.manual_schedule())

        ones = const.tile([P, 1], F32, name="ones")
        nc.vector.memset(ones[:], 1.0)
        b_bf = const.tile([P, H, 2], BF16, name="b_bf")
        scr = const.tile([P, 1], F32, name="scr")
        nc.scalar.activation(out=scr[:], in_=ones[:], func=ACT.Sin, scale=1.0)

        ident = const.tile([P, P], F32, name="ident")
        make_identity(nc, ident[:])
        n_iota = const.tile([P, HALF], F32, name="n_iota")
        nc.gpsimd.iota(n_iota[:], pattern=[[1, 4], [4, P]], base=0,
                       channel_multiplier=0, allow_small_or_imprecise_dtypes=True)

        xv = x[0].rearrange("(s r i) k -> s i r k", s=2, i=4)
        x_raw = {}
        head_src = {}

        def load_x(s, i):
            t = const.tile([P, E], BF16, name="x_raw%d%d" % (s, i))
            nc.sync.dma_start(out=t[:], in_=xv[s, i])
            x_raw[(s, i)] = t

        def load_w(c, g):
            h0, nh = CHUNKS[c]
            t = const.tile([P, 4, D * nh], BF16, name="w_raw%d%d" % (c, g))
            nc.sync.dma_start(
                out=t[:],
                in_=w[512 * g:512 * (g + 1), D * h0:D * (h0 + nh)].rearrange("(p j) c -> p j c", j=4))
            for hl in range(nh):
                head_src[(h0 + hl, g)] = t[:, :, D * hl:D * (hl + 1)]

        for i in range(4):
            load_x(0, i)
        load_x(1, 0)
        load_x(1, 1)
        load_w(0, 0)
        nc.sync.dma_start(out=b_bf[:], in_=b.rearrange("(h j e) -> j h e", h=H, e=2))
        for g in range(1, G):
            load_w(0, g)
        load_x(1, 2)
        load_x(1, 3)
        for c in range(1, len(CHUNKS)):
            for g in range(G):
                load_w(c, g)

        ratio = 10000.0 ** (-1.0 / 127.0)
        frow = const.tile([P, P], F32, name="frow")
        for m in range(4):
            nc.vector.tensor_scalar(out=frow[:, m:m + 1], in0=ones[:], scalar1=ratio ** m / (2.0 * math.pi),
                                    scalar2=None, op0=ALU.mult)
        for m in range(4, 16, 4):
            nc.vector.tensor_scalar(out=frow[:, m:m + 4], in0=frow[:, 0:4], scalar1=ratio ** m,
                                    scalar2=None, op0=ALU.mult)
        for m in range(16, P, 16):
            nc.vector.tensor_scalar(out=frow[:, m:m + 16], in0=frow[:, 0:16], scalar1=ratio ** m,
                                    scalar2=None, op0=ALU.mult)
        fdiag = const.tile([P, P], F32, name="fdiag")
        fcol = const.tile([P, 1], F32, name="fcol")
        nc.vector.scalar_tensor_tensor(out=fdiag[:], in0=frow[:], scalar=1.0, in1=ident[:], op0=ALU.mult, op1=ALU.mult,
                                       accum_out=fcol[:])

        xg = const.tile([P, G, 4 * HALF], BF16, name="xg", align_bytes=64)
        xg_w = xg[:].bitcast(F32).rearrange("p g (i r u) -> p g i r u", i=4, u=2)
        xc = [const.tile([P, G, HALF], U32, name="xc%d" % s, align_bytes=64) for s in range(2)]
        xs = [const.tile([P, G, HALF], U8, name="xs%d" % s, align_bytes=64) for s in range(2)]
        xts = {}

        def x_transposes(s, i):
            words = x_raw[(s, i)][:].bitcast(F32)
            for a in range(2):
                xt = tp_pool.tile([P, 2, 2, P], F32, name="xt", tag="tp")
                for gg in range(2):
                    g = 2 * a + gg
                    for u in range(2):
                        nc.tensor.transpose(xt[:, gg, u, :], words[:, 256 * g + u:256 * (g + 1):2], ident[:])
                xts[(s, i, a)] = xt

        def x_copy(s, i, a, eng):
            dst = xg_w[:, 2 * a:2 * a + 2, i, :, :]
            src = xts[(s, i, a)][:].rearrange("p g u r -> p g r u")
            if eng == "s":
                nc.scalar.copy(out=dst, in_=src)
            else:
                nc.vector.tensor_copy(out=dst, in_=src)

        def x_quant(s, i):
            c = slice(P * i, P * (i + 2))
            for g in range(G):
                nc.vector.quantize_mx(out=xc[s][:, g, c].bitcast(E5X4), scales=xs[s][:, g, c],
                                      in_=xg[:, g, 512 * i:512 * (i + 2)])

        w_codes = {}
        wg_tiles = {}

        def w_interleave(h, g, eng):
            if (h, g // 2) not in wg_tiles:
                wg_tiles[(h, g // 2)] = wg_pool.tile([P, 2, 4 * D], BF16, name="wg", tag="wg", align_bytes=64)
            t = wg_tiles[(h, g // 2)]
            dst = t[:, g % 2, :].rearrange("p (e j i t) -> p e j t i", e=2, i=4, t=4)
            src = head_src[(h, g)].rearrange("p t (j i e) -> p e j t i", e=2, i=4)
            if eng == "s":
                nc.scalar.copy(out=dst, in_=src)
            elif eng == "v":
                nc.vector.tensor_copy(out=dst, in_=src)
            else:
                for e in range(2):
                    nc.gpsimd.tensor_scalar(out=dst[:, e], in0=src[:, e], scalar1=1.0, scalar2=0.0,
                                            op0=ALU.mult, op1=ALU.add)

        def w_tiles(h):
            cod = wc_pool.tile([P, G, D], U32, name="wcod", tag="wcod", align_bytes=64)
            sca = wc_pool.tile([P, G, D], U8, name="wsca", tag="wsca", align_bytes=64)
            w_codes[h] = (cod, sca)

        def w_quant1(h, g):
            cod, sca = w_codes[h]
            nc.vector.quantize_mx(out=cod[:, g, :].bitcast(E4X4), scales=sca[:, g, :],
                                  in_=wg_tiles[(h, g // 2)][:, g % 2, :])

        def w_quant2(h, a):
            cod, sca = w_codes[h]
            nc.vector.quantize_mx(
                out=cod[:, 2 * a:2 * a + 2, :].rearrange("p g c -> p (g c)").bitcast(E4X4),
                scales=sca[:, 2 * a:2 * a + 2, :].rearrange("p g c -> p (g c)"),
                in_=wg_tiles[(h, a)][:].rearrange("p g c -> p (g c)"))

        table = const.tile([P, 2, 2, HALF], F32, name="table")
        turns = const.tile([P, N_TOK], F32, name="turns")
        b_f = const.tile([P, H, 2], F32, name="b_f")

        whole_i = const.tile([P, HALF], I32, name="whole_i")
        step_i = const.tile([P, 1], I32, name="step_i")
        step_t = const.tile([P, 1], F32, name="step_t")

        def tables_vector0():
            nc.vector.tensor_scalar(out=whole_i[:], in0=n_iota[:], scalar1=fcol[:, 0:1], scalar2=None, op0=ALU.mult)
            nc.vector.tensor_scalar(out=step_i[:], in0=fcol[:], scalar1=float(HALF), scalar2=None, op0=ALU.mult)
            nc.vector.scalar_tensor_tensor(out=turns[:, 0:HALF], in0=n_iota[:], scalar=fcol[:, 0:1], in1=whole_i[:],
                                           op0=ALU.mult, op1=ALU.subtract)
            nc.vector.scalar_tensor_tensor(out=step_t[:], in0=fcol[:], scalar=float(HALF), in1=step_i[:],
                                           op0=ALU.mult, op1=ALU.subtract)

        def tables_vector1():
            nc.vector.tensor_scalar(out=whole_i[:], in0=turns[:, 0:HALF], scalar1=step_t[:, 0:1], scalar2=None, op0=ALU.add)
            nc.vector.scalar_tensor_tensor(out=turns[:, HALF:N_TOK], in0=turns[:, 0:HALF], scalar=step_t[:, 0:1], in1=whole_i[:],
                                           op0=ALU.add, op1=ALU.subtract)

        def tables_sin(s):
            c = slice(HALF * s, HALF * (s + 1))
            nc.scalar.activation(out=table[:, s, 1, :], in_=turns[:, c], func=ACT.Sin, scale=2.0 * math.pi)

        def tables_abs(s):
            c = slice(HALF * s, HALF * (s + 1))
            nc.scalar.activation(out=table[:, s, 0, :], in_=turns[:, c], func=ACT.Abs)

        def tables_cos(s):
            c = slice(HALF * s, HALF * (s + 1))
            nc.scalar.activation(out=table[:, s, 0, :], in_=table[:, s, 0, :], func=ACT.Sin, scale=-2.0 * math.pi, bias=0.5 * math.pi)

        def bias_columns():
            nc.vector.tensor_copy(out=b_f[:], in_=b_bf[:])

        accs = {}
        rot = {}
        ots = {}

        def mx_one(t, e, g):
            h, s = UNITS[t]
            cod, sca = w_codes[h]
            if g == 0:
                accs[(t, e)] = acc_pool.tile([P, HALF], F32, name="acc", tag="acc")
            nc.tensor.matmul_mx(
                out=accs[(t, e)][:],
                lhsT=cod[:, g, P * e:P * (e + 1)].bitcast(E4X4),
                lhsT_scale=sca[:, g, P * e:P * (e + 1)],
                rhs=xc[s][:, g, :].bitcast(E5X4),
                rhs_scale=xs[s][:, g, :],
                start=(g == 0), stop=(g == G - 1))

        def mx_pass(t, g):
            for e in range(2):
                mx_one(t, e, g)

        def mx_bank(t, e):
            for g in range(G):
                mx_one(t, e, g)

        def rotated(t, e):
            if (t, e) not in rot:
                rot[(t, e)] = ep3.tile([P, 2, HALF], F32, name="rot%d" % e, tag="rot%d" % e)
            return rot[(t, e)]

        def product(t, e, k):
            h, s = UNITS[t]
            nc.vector.scalar_tensor_tensor(out=rotated(t, e)[:, k, :], in0=accs[(t, e)][:], scalar=b_f[:, h, e:e + 1],
                                           in1=table[:, s, k, :], op0=ALU.add, op1=ALU.mult)

        def products(t, e, c0=0, c1=HALF):
            h, s = UNITS[t]
            nc.vector.scalar_tensor_tensor(out=rotated(t, e)[:, :, c0:c1],
                                           in0=accs[(t, e)][:, c0:c1].unsqueeze(1).to_broadcast([P, 2, c1 - c0]),
                                           scalar=b_f[:, h, e:e + 1], in1=table[:, s, :, c0:c1], op0=ALU.add, op1=ALU.mult)

        def subtract(t, eng, c0=0, c1=HALF):
            ec, os_ = rot[(t, 0)][:, 0, c0:c1], rot[(t, 1)][:, 1, c0:c1]
            eng.tensor_tensor(out=ec, in0=ec, in1=os_, op=ALU.subtract)

        def add(t, eng, c0=0, c1=HALF):
            oc, es = rot[(t, 1)][:, 0, c0:c1], rot[(t, 0)][:, 1, c0:c1]
            eng.tensor_tensor(out=oc, in0=oc, in1=es, op=ALU.add)

        def out_transposes(t, a):
            ec, es, oc = rot[(t, 0)][:, 0, :], rot[(t, 0)][:, 1, :], rot[(t, 1)][:, 0, :]
            ot = tp_pool.tile([P, 2, 2, P], F32, name="ot", tag="tp")
            for ii in range(2):
                i = 2 * a + ii
                nc.tensor.transpose(ot[:, ii, 0, :], ec[:, P * i:P * (i + 1)], ident[:])
                if GP_ODD_FROM <= t < LAST:
                    nc.tensor.transpose(ot[:, ii, 1, :], oc[:, P * i:P * (i + 1)], ident[:])
                else:
                    nc.tensor.matmul(ot[:, ii, 1, :], lhsT=oc[:, P * i:P * (i + 1)], rhs=ident[:],
                                     is_transpose=True, start=True, stop=False)
                    nc.tensor.matmul(ot[:, ii, 1, :], lhsT=es[:, P * i:P * (i + 1)], rhs=ident[:],
                                     is_transpose=True, start=False, stop=True)
            ots[(t, a)] = ot

        results = {}

        def out_copy(t, a, eng="s"):
            if a == 0:
                results[t] = res_pool.tile([P, 4, D], F32, name="res", tag="res")
            dst = results[t][:, 2 * a:2 * a + 2, :].rearrange("p i (j e) -> p i j e", e=2)
            src = ots[(t, a)][:].rearrange("p i e j -> p i j e")
            if eng == "s":
                nc.scalar.copy(out=dst, in_=src)
            else:
                nc.vector.tensor_copy(out=dst, in_=src)

        def out_store(t):
            h, s = UNITS[t]
            nc.sync.dma_start(
                out=out[0, h, HALF * s:HALF * (s + 1), :].rearrange("(r i) d -> r (i d)", i=4),
                in_=results[t][:].rearrange("p i d -> p (i d)"))

        def out_store_half(t, a):
            h, s = UNITS[t]
            nc.sync.dma_start(
                out=out[0, h, HALF * s:HALF * (s + 1), :].rearrange("(r a i) d -> r a (i d)", a=2, i=2)[:, a, :],
                in_=results[t][:, 2 * a:2 * a + 2, :].rearrange("p i d -> p (i d)"))

        tables_vector0()
        tables_sin(0)
        tables_vector1()
        w_tiles(0)
        w_tiles(1)
        x_transposes(0, 0)
        x_transposes(0, 1)
        for i in range(4):
            x_copy(0, i, 0, "s")
            x_copy(0, i, 1, "v" if i in (1, 2) else "s")
            if i + 2 < 4:
                x_transposes(0, i + 2)
            if i == 1:
                tables_abs(0)
            if i == 2:
                tables_cos(0)
            if i == 3:
                w_interleave(0, 0, "v")
            if i % 2 == 1:
                x_quant(0, i - 1)
        x_transposes(1, 0)
        w_interleave(1, 0, "s")
        x_transposes(1, 1)
        x_copy(1, 0, 0, "s")
        x_copy(1, 0, 1, "s")
        for g in range(G):
            if g > 0:
                w_interleave(0, g, "v")
                w_interleave(1, g, "s")
                w_quant1(1, g - 1)
                mx_pass(1, g - 1)
            w_quant1(0, g)
            mx_pass(0, g)
            if g == 1:
                x_copy(1, 1, 0, "s")
                x_copy(1, 1, 1, "s")
            if g == 2:
                x_quant(1, 0)
        x_transposes(1, 2)
        w_quant1(1, G - 1)
        mx_pass(1, G - 1)
        x_transposes(1, 3)
        tables_sin(1)
        tables_abs(1)
        bias_columns()
        product(0, 0, 0)
        product(0, 1, 1)
        x_copy(1, 2, 0, "s")
        x_copy(1, 2, 1, "s")
        subtract(0, nc.gpsimd)
        product(0, 0, 1)
        product(0, 1, 0)
        tables_cos(1)
        x_copy(1, 3, 0, "s")
        x_copy(1, 3, 1, "s")
        x_quant(1, 2)
        out_transposes(0, 0)
        out_transposes(0, 1)
        product(1, 0, 0)
        product(1, 1, 1)
        subtract(1, nc.gpsimd)
        product(1, 0, 1)
        product(1, 1, 0)
        units = len(UNITS)
        queue = dict((k, [(h, g) for h in range(2, H) for g in range(G) if WI_ENGINE[h - 2][g] == k]) for k in "svg")
        done = []
        quantised = set()

        def prep(k, t=2):
            if queue[k] and queue[k][0][0] <= (t + LEAD) // 2:
                h, g = queue[k].pop(0)
                w_interleave(h, g, k)
                done.append((h, g))

        def quant_ready():
            for h in range(2, H):
                for a in range(2):
                    if (h, a) not in quantised and (h, 2 * a) in done and (h, 2 * a + 1) in done:
                        if a == 0:
                            w_tiles(h)
                        w_quant2(h, a)
                        quantised.add((h, a))
                        return

        for g in range(G):
            prep("s")
        quant_ready()
        for t in range(2, units + 2):
            if t < PAIR_FROM:
                multiply, transpose = (t,), (t - 2,)
            elif t < LAST - 1:
                multiply, transpose = ((t, t + 1), (t - 2, t - 1)) if t % 2 == 0 else ((), ())
            elif t <= LAST:
                multiply, transpose = (t,), (t - 2,)
            else:
                multiply, transpose = (), (t - 2,)
            for u in multiply:
                mx_bank(u, 0)
                mx_bank(u, 1)
            for u in transpose:
                if u > 0:
                    out_transposes(u, 0)
                    out_transposes(u, 1)
            if t < LAST:
                products(t, 0)
                product(t, 1, 1)
                quant_ready()
                prep("v", t)
                subtract(t, nc.gpsimd)
                product(t, 1, 0)
                if t >= GP_ODD_FROM:
                    add(t, nc.gpsimd)
            elif t == LAST:
                products(t, 0)
                for c in (0, 256):
                    products(t, 1, c, c + 256)
                    subtract(t, nc.vector, c, c + 256)
            out_copy(t - 2, 0)
            if t - 2 == LAST:
                out_store_half(t - 2, 0)
            prep("s", t)
            out_copy(t - 2, 1, "v" if t - 2 == LAST else "s")
            if t - 2 == LAST:
                out_store_half(t - 2, 1)
            else:
                out_store(t - 2)
            prep("s", t)
